import numpy as np
import ml_dtypes


def mxq(x, axis, fmt="e4m3"):
    dtype, down = {"e4m3": (ml_dtypes.float8_e4m3fn, 7), "e5m2": (ml_dtypes.float8_e5m2, 14)}[fmt]
    v = np.moveaxis(np.asarray(x, np.float32).astype(ml_dtypes.bfloat16).astype(np.float64), axis, -1)
    blocks = v.reshape(v.shape[:-1] + (-1, 32))
    amax = np.abs(blocks).max(-1, keepdims=True)
    byte = np.maximum(np.where(amax > 0, np.frexp(amax)[1] - 1 + 127, 0) - down, 1)
    scale = np.exp2(byte - 127.0)
    codes = (blocks / scale).astype(np.float32).astype(dtype).astype(np.float64)
    return np.moveaxis((codes * scale).reshape(v.shape), -1, axis)


WIDE = False


def mx_kscale(k):
    if not WIDE:
        return np.ones(k)
    levels = np.array([18, -18])
    if k % 512:
        return np.exp2(np.random.permutation(np.resize(levels, k // 32))).repeat(32)
    a = np.empty((k // 512, 16))
    for p in range(k // 512):
        a[p, :8] = np.random.permutation(np.resize(levels, 8))
        for g in range(8):
            far = levels[np.abs(levels - a[p, g]) >= 10]
            a[p, g + 8] = far[np.random.randint(len(far))]
    return np.exp2(a.ravel()).repeat(32)


BF16 = ml_dtypes.bfloat16


def bf(x):
    return np.asarray(x, np.float32).astype(BF16)


def f64(x):
    return np.asarray(x).astype(np.float64)


S, D, H, DH, F = 512, 1024, 8, 128, 3072
E = H * DH
EPS = 1e-5
XS = 0.015


def gelu_tanh_grad(v):
    c = np.sqrt(2.0 / np.pi)
    t = np.tanh(c * (v + 0.044715 * v**3))
    return 0.5 * (1.0 + t) + 0.5 * v * (1.0 - t * t) * c * (1.0 + 3.0 * 0.044715 * v**2)


def setup_inputs():
    s = np.maximum(mx_kscale(S), 1.0)[:, None]
    u = mx_kscale(D)
    v = mx_kscale(F)
    x = np.random.standard_normal((S, D)) + 0.5 * np.random.standard_normal(S)[:, None]
    x0 = bf(XS * x[None])
    attn_vec = bf(np.random.standard_normal((S, E)) * 0.6)
    ln_scale = bf(1.0 + 0.1 * np.random.standard_normal(D))
    ln_offset = bf(0.1 * np.random.standard_normal(D))
    Wo = bf(np.random.standard_normal((E, D)) / np.sqrt(E))
    W1_0 = bf(np.random.standard_normal((D, F)) / np.sqrt(D))
    b1 = bf(0.1 * np.random.standard_normal(F))
    W2_0 = bf(np.random.standard_normal((F, D)) / np.sqrt(F))
    b2 = bf(0.1 * np.random.standard_normal(D))
    g = bf(np.random.standard_normal((1, S, D)) * np.exp2(np.random.randint(-6, 1, (1, S, 1))) / s * u)
    xf = f64(x0)
    mean = xf.mean(axis=-1, keepdims=True)
    rstd = 1.0 / np.sqrt(xf.var(axis=-1, keepdims=True) + EPS)
    z1 = (f64(ln_scale) * ((xf - mean) * rstd) + f64(ln_offset)) @ f64(W1_0) + f64(b1)
    return {"x": bf(xf * s),
            "attn_vec": attn_vec,
            "ln_scale": ln_scale,
            "ln_offset": ln_offset,
            "Wo": Wo,
            "W1": bf(f64(W1_0) / v),
            "b1": b1,
            "W2": bf(f64(W2_0) * v[:, None] / u),
            "b2": b2,
            "z1": np.asarray(z1, np.float32),
            "mean": np.asarray(mean, np.float32),
            "rstd": np.asarray(rstd, np.float32),
            "grad_out": g}


def reference(x, attn_vec, ln_scale, ln_offset, Wo, W1, b1, W2, b2, z1, mean, rstd, grad_out):
    g = f64(grad_out)[0]
    r = f64(rstd)[0]
    sc = f64(ln_scale)
    xhat = (f64(x)[0] - f64(mean)[0]) * r
    xn = sc * xhat + f64(ln_offset)
    dh = mxq(g, 1, "e5m2") @ mxq(f64(W2), 1, "e4m3").T
    dz1 = dh * gelu_tanh_grad(f64(z1)[0])
    dxn = mxq(dz1, 1, "e5m2") @ mxq(f64(W1), 1, "e4m3").T
    dW1 = mxq(xn, 0, "e4m3").T @ mxq(dz1, 0, "e5m2")
    a = dxn * sc
    dx = r * (a - a.mean(axis=1, keepdims=True) - xhat * (a * xhat).mean(axis=1, keepdims=True))
    return dx[None], dW1

@@ -1,0 +1,518 @@
+from contextlib import ExitStack
+
+import concourse.mybir as mybir
+from concourse.masks import make_identity
+
+S, D, F = 512, 1024, 3072
+FLOPS = 3 * 2 * S * D * F
+BYTES = 2 * (2 * S * D + 2 * D * F) + 4 * (S * F + S * D + D * F)
+
+F32 = mybir.dt.float32
+BF16 = mybir.dt.bfloat16
+U32 = mybir.dt.uint32
+U8 = mybir.dt.uint8
+E4M3 = mybir.dt.float8_e4m3fn_x4
+E5M2 = mybir.dt.float8_e5m2_x4
+ADD = mybir.AluOpType.add
+SUB = mybir.AluOpType.subtract
+MUL = mybir.AluOpType.mult
+ACT = mybir.ActivationFunctionType
+
+P = 128
+FC = 512
+NCH = F // FC
+LAG = 2
+
+A = 0.044715
+C = math_c = (2.0 / 3.141592653589793) ** 0.5
+BETA = 3.0 * A * C
+SQ_SCALE = BETA**0.5
+
+
+def tile_transformerlayershard_pb_v_kernel(
+    tc, x, attn_vec, ln_scale, ln_offset, wo, w1, b1, w2, b2, z1, mean, rstd, grad_out, out_0, out_1
+):
+    nc = tc.nc
+    x_v = x[0].rearrange("(p j) d -> p j d", j=4)
+    g_v = grad_out[0].rearrange("(p j) d -> p j d", j=4)
+    z1_v = z1[0].rearrange("(p j) f -> p j f", j=4)
+    mean_v = mean[0].rearrange("(p j) o -> p (j o)", j=4)
+    rstd_v = rstd[0].rearrange("(p j) o -> p (j o)", j=4)
+    w1_v = w1.rearrange("(m p) f -> p m f", p=P)
+    w2_v = w2.rearrange("(m p) d -> p m d", p=P)
+    o0_v = out_0[0].rearrange("(p j) d -> p j d", j=4)
+    o1_v = out_1.rearrange("(m p) f -> p m f", p=P)
+
+    with ExitStack() as ctx:
+        sb = ctx.enter_context(tc.tile_pool(name="sb", bufs=1))
+        ps = ctx.enter_context(tc.psum_pool(name="ps", bufs=1))
+
+        def st(shape, dtype, tag, bufs):
+            return sb.tile(shape, dtype, name=tag, tag=tag, bufs=bufs, align_bytes=64)
+
+        def bank(tag, bufs):
+            return ps.tile([P, 512], F32, name=tag, tag=tag, bufs=bufs)
+
+        def tp_bank():
+            return bank("tp", 3)
+
+        def dh_bank():
+            return bank("dh", 3)
+
+        def dw_bank():
+            return bank("dw", 2)
+
+        ident_f = st([P, P], F32, "ident_f", 1)
+        ident_b = st([P, P], BF16, "ident_b", 1)
+        vec = st([P, D], BF16, "vec", 1)
+        sc = st([P, D], BF16, "sc", 1)
+        off = st([P, D], BF16, "off", 1)
+        x_sb = st([P, 4, D], BF16, "x_sb", 1)
+        mean_sb = st([P, 4], F32, "mean_sb", 1)
+        rstd_sb = st([P, 4], F32, "rstd_sb", 1)
+        nmean = st([P, 4], F32, "nmean", 1)
+        k1 = st([P, 4], F32, "k1", 1)
+        r2 = st([P, 4], F32, "r2", 1)
+        k3 = st([P, 4], F32, "k3", 1)
+        warm = st([P, 1], F32, "warm", 1)
+        gq = st([P, 2, S], U32, "gq", 1)
+        gs = st([P, 2, S], U8, "gs", 1)
+        xnq = st([P, D], U32, "xnq", 1)
+        xns = st([P, D], U8, "xns", 1)
+
+        z1t, w1t, w2t = {}, {}, {}
+        sqt, qt, get, xt = {}, {}, {}, {}
+        w2g, w2q, w2s = {}, {}, {}
+        w1g, w1q, w1s = {}, {}, {}
+        dht, ht, dzt, dzi = {}, {}, {}, {}
+        dzq, dzs, dtg, dtq, dts = {}, {}, {}, {}, {}
+        stage = {}
+
+        def load_z1(c, h):
+            t = st([P, 2, FC], F32, "z1t", 4)
+            nc.sync.dma_start(out=t[:], in_=z1_v[:, 2 * h : 2 * h + 2, c * FC : (c + 1) * FC])
+            z1t[c, h] = t
+
+        def load_w2(c):
+            t = st([P, 4, D], BF16, "w2t", 2)
+            for i in range(2):
+                nc.sync.dma_start(
+                    out=t[:, 2 * i : 2 * i + 2, :], in_=w2_v[:, 4 * c + 2 * i : 4 * c + 2 * i + 2, :]
+                )
+            w2t[c] = t
+
+        def load_w1(c):
+            t = st([P, 8, FC], BF16, "w1t", 2)
+            nc.sync.dma_start(out=t[:], in_=w1_v[:, :, c * FC : (c + 1) * FC])
+            w1t[c] = t
+
+        def sq(c, h):
+            t = st([P, 1024], F32, "sq", 2)
+            nc.scalar.activation(
+                out=t[:], in_=z1t[c, h][:].rearrange("p j f -> p (j f)"), func=ACT.Square, scale=SQ_SCALE
+            )
+            sqt[c, h] = t
+
+        def qq(c, h):
+            t = st([P, 1024], F32, "qt", 4)
+            nc.vector.scalar_tensor_tensor(
+                out=t[:], in0=sqt[c, h][:], scalar=BETA / A, in1=z1t[c, h][:].rearrange("p j f -> p (j f)"),
+                op0=ADD, op1=MUL,
+            )
+            qt[c, h] = t
+
+        def th(c, h):
+            t = qt[c, h]
+            nc.scalar.activation(out=t[:], in_=t[:], func=ACT.Tanh, scale=-A * C / BETA)
+
+        def ge(c, h):
+            t = st([P, 1024], F32, "ge", 2)
+            nc.scalar.activation(
+                out=t[:], in_=z1t[c, h][:].rearrange("p j f -> p (j f)"), func=ACT.Gelu_apprx_tanh, scale=-1.0
+            )
+            get[c, h] = t
+
+        def xx(c, h):
+            t = st([P, 1024], F32, "xt", 4)
+            nc.vector.scalar_tensor_tensor(
+                out=t[:], in0=sqt[c, h][:], scalar=BETA / (3.0 * A), in1=get[c, h][:], op0=ADD, op1=MUL
+            )
+            xt[c, h] = t
+
+        def grp():
+            return st([P, 512, 4], BF16, "grp", 5)
+
+        def evac(eng, dst, r0, bk):
+            out = dst[:, r0 : r0 + 256, :].rearrange("p r j -> p (r j)").bitcast(F32)
+            out = out.rearrange("p (m r u) -> p m r u", m=2, u=2)
+            src = bk[:].rearrange("p (m u r) -> p m r u", m=2, u=2)
+            if eng == "v":
+                nc.vector.tensor_copy(out=out, in_=src)
+            else:
+                nc.scalar.copy(out=out, in_=src)
+
+        def transposes(eng, srcs, dst, r0):
+            bk = tp_bank()
+            for i in range(2):
+                words = srcs[i].bitcast(F32)
+                for u in range(2):
+                    nc.tensor.transpose(
+                        bk[:, (2 * i + u) * P : (2 * i + u + 1) * P], words[:, u:256:2], ident_f[:]
+                    )
+            evac(eng, dst, r0, bk)
+
+        def quant(codes, scales, g, fmt):
+            nc.vector.quantize_mx(
+                out=codes.bitcast(fmt), scales=scales, in_=g[:].rearrange("p r j -> p (r j)")
+            )
+
+        def t2(c, b, eng):
+            k, mp = divmod(b, 2)
+            if mp == 0:
+                w2g[c, k] = grp()
+            if b == 0:
+                w2q[c] = st([P, 2, FC], U32, "w2q", 2)
+                w2s[c] = st([P, 2, FC], U8, "w2s", 2)
+            srcs = [w2t[c][:, 2 * mp + i, 512 * k : 512 * (k + 1)] for i in range(2)]
+            transposes(eng, srcs, w2g[c, k], 256 * mp)
+
+        def qw2(c, k):
+            quant(w2q[c][:, k, :], w2s[c][:, k, :], w2g[c, k], E4M3)
+
+        def t1(c, b, eng):
+            h, mp = divmod(b, 2)
+            if mp == 0:
+                w1g[c, h] = grp()
+            if b == 0:
+                w1q[c] = st([P, D], U32, "w1q", NCH)
+                w1s[c] = st([P, D], U8, "w1s", NCH)
+            srcs = [w1t[c][:, 4 * h + 2 * mp + i, :] for i in range(2)]
+            transposes(eng, srcs, w1g[c, h], 256 * mp)
+
+        def qw1(c, h):
+            cols = slice(512 * h, 512 * (h + 1))
+            quant(w1q[c][:, cols], w1s[c][:, cols], w1g[c, h], E4M3)
+
+        def dh(c, t):
+            bk = dh_bank()
+            for k in range(2):
+                nc.tensor.matmul_mx(
+                    out=bk[:],
+                    lhsT=gq[:, k, P * t : P * (t + 1)].bitcast(E5M2),
+                    lhsT_scale=gs[:, k, P * t : P * (t + 1)],
+                    rhs=w2q[c][:, k, :].bitcast(E4M3),
+                    rhs_scale=w2s[c][:, k, :],
+                    start=(k == 0),
+                    stop=(k == 1),
+                )
+            dht[c, t] = bk
+
+        def hh(c, t):
+            h, i = divmod(t, 2)
+            if i == 0:
+                ht[c, h] = st([P, 1024], F32, "hh", 2)
+            cols = slice(512 * i, 512 * (i + 1))
+            nc.vector.scalar_tensor_tensor(
+                out=ht[c, h][:, cols], in0=qt[c, h][:, cols], scalar=-1.0, in1=dht[c, t][:], op0=ADD, op1=MUL
+            )
+
+        def dz(c, h):
+            if h == 0:
+                dzt[c] = st([P, 4, FC], BF16, "dz", 2)
+            nc.vector.scalar_tensor_tensor(
+                out=dzt[c][:, 2 * h : 2 * h + 2, :].rearrange("p j f -> p (j f)"),
+                in0=xt[c, h][:], scalar=-0.5, in1=ht[c, h][:], op0=ADD, op1=MUL,
+            )
+
+        def interleave(src):
+            g = grp()
+            nc.vector.tensor_copy(out=g[:], in_=src[:].rearrange("p j f -> p f j"))
+            return g
+
+        def il(c):
+            dzi[c] = interleave(dzt[c])
+
+        def qdz(c):
+            dzq[c] = st([P, FC], U32, "dzq", 3)
+            dzs[c] = st([P, FC], U8, "dzs", 3)
+            quant(dzq[c][:], dzs[c][:], dzi[c], E5M2)
+
+        def t3(c, b, eng):
+            if b == 0:
+                dtg[c] = grp()
+            srcs = [dzt[c][:, 2 * b + i, :] for i in range(2)]
+            transposes(eng, srcs, dtg[c], 256 * b)
+
+        def qdt(c):
+            dtq[c] = st([P, S], U32, "dtq", NCH)
+            dts[c] = st([P, S], U8, "dts", NCH)
+            quant(dtq[c][:], dts[c][:], dtg[c], E5M2)
+
+        def dw(c, m, eng):
+            bk = dw_bank()
+            nc.tensor.matmul_mx(
+                out=bk[:],
+                lhsT=xnq[:, P * m : P * (m + 1)].bitcast(E4M3),
+                lhsT_scale=xns[:, P * m : P * (m + 1)],
+                rhs=dzq[c][:].bitcast(E5M2),
+                rhs_scale=dzs[c][:],
+                start=True,
+                stop=True,
+            )
+            if m % 2 == 0:
+                stage[c, m] = st([P, 2, FC], F32, "stage", 3)
+            t = stage[c, m - m % 2]
+            if eng == "v":
+                nc.vector.tensor_copy(out=t[:, m % 2, :], in_=bk[:])
+            else:
+                nc.scalar.copy(out=t[:, m % 2, :], in_=bk[:])
+            if m % 2 == 1:
+                nc.sync.dma_start(out=o1_v[:, m - 1 : m + 1, c * FC : (c + 1) * FC], in_=t[:])
+
+        xna = {}
+
+        def xn_a(h, t):
+            if t % 2 == 0:
+                xna[h, t // 2] = st([P, 1024], F32, "hh", 2)
+            a = xna[h, t // 2]
+            nc.vector.scalar_tensor_tensor(
+                out=a[:, 512 * (t % 2) : 512 * (t % 2 + 1)], in0=x_sb[:, t, 512 * h : 512 * (h + 1)],
+                scalar=mean_sb[:, t : t + 1], in1=sc[:, 512 * h : 512 * (h + 1)], op0=SUB, op1=MUL,
+            )
+
+        xnb = {}
+
+        def xn_b(h, t):
+            if t == 0:
+                xnb[h] = st([P, 4, 512], BF16, "xn", 1)
+            a = xna[h, t // 2]
+            nc.vector.scalar_tensor_tensor(
+                out=xnb[h][:, t, :], in0=a[:, 512 * (t % 2) : 512 * (t % 2 + 1)],
+                scalar=rstd_sb[:, t : t + 1], in1=off[:, 512 * h : 512 * (h + 1)], op0=MUL, op1=ADD,
+            )
+
+        def xn_elem(h):
+            xn_a(h, 0)
+            xn_a(h, 1)
+            xn_b(h, 0)
+            xn_a(h, 2)
+            xn_b(h, 1)
+            xn_a(h, 3)
+            xn_b(h, 2)
+            xn_b(h, 3)
+
+        xni = {}
+
+        def xn_il(h):
+            xni[h] = interleave(xnb[h])
+
+        def xn_q(h):
+            cols = slice(512 * h, 512 * (h + 1))
+            quant(xnq[:, cols], xns[:, cols], xni[h], E4M3)
+
+        dxt = {}
+
+        def dxn(t, h, c0, c1):
+            if c0 == 0:
+                dxt[t, h] = dh_bank() if h == 0 else tp_bank()
+            for c in range(c0, c1):
+                nc.tensor.matmul_mx(
+                    out=dxt[t, h][:],
+                    lhsT=dtq[c][:, P * t : P * (t + 1)].bitcast(E5M2),
+                    lhsT_scale=dts[c][:, P * t : P * (t + 1)],
+                    rhs=w1q[c][:, 512 * h : 512 * (h + 1)].bitcast(E4M3),
+                    rhs_scale=w1s[c][:, 512 * h : 512 * (h + 1)],
+                    start=(c == 0),
+                    stop=(c == NCH - 1),
+                )
+
+        at, tmpt, sums = {}, {}, {}
+
+        def ep_a(t, h):
+            if h == 0:
+                at[t] = st([P, D], F32, "qt", 4)
+                sums[t] = st([P, 8], F32, "sums", 4)
+            cols = slice(512 * h, 512 * (h + 1))
+            nc.vector.scalar_tensor_tensor(
+                out=at[t][:, cols], in0=dxt[t, h][:], scalar=1.0, in1=sc[:, cols], op0=MUL, op1=MUL,
+                accum_out=sums[t][:, h : h + 1],
+            )
+
+        def ep_b(t):
+            junk = st([P, D], F32, "sq", 2)
+            nc.vector.scalar_tensor_tensor(
+                out=junk[:], in0=x_sb[:, t, :], scalar=mean_sb[:, t : t + 1], in1=at[t][:], op0=SUB, op1=MUL,
+                accum_out=sums[t][:, 2:3],
+            )
+
+        def ep_c(t):
+            s = sums[t]
+            nc.vector.scalar_tensor_tensor(
+                out=s[:, 3:4], in0=s[:, 0:1], scalar=s[:, 1:2], in1=k1[:, t : t + 1], op0=ADD, op1=MUL
+            )
+            nc.vector.tensor_tensor(out=s[:, 4:5], in0=s[:, 2:3], in1=k3[:, t : t + 1], op=MUL)
+            nc.vector.scalar_tensor_tensor(
+                out=s[:, 5:6], in0=s[:, 4:5], scalar=nmean[:, t : t + 1], in1=s[:, 3:4], op0=MUL, op1=ADD
+            )
+            tmpt[t] = st([P, D], F32, "ge", 2)
+            nc.scalar.activation(
+                out=tmpt[t][:], in_=x_sb[:, t, :], func=ACT.Identity, scale=s[:, 4:5], bias=s[:, 5:6]
+            )
+
+        def ep_d(t):
+            o = st([P, D], F32, "xt", 4)
+            nc.vector.scalar_tensor_tensor(
+                out=o[:], in0=at[t][:], scalar=rstd_sb[:, t : t + 1], in1=tmpt[t][:], op0=MUL, op1=SUB
+            )
+            nc.sync.dma_start(out=o0_v[:, t, :], in_=o[:])
+
+        load_z1(0, 0)
+        g_sb = st([P, 4, D], BF16, "w2t", 2)
+        for i in range(2):
+            nc.sync.dma_start(out=g_sb[:, 2 * i : 2 * i + 2, :], in_=g_v[:, 2 * i : 2 * i + 2, :])
+        load_z1(0, 1)
+        load_w2(0)
+        nc.vector.memset(warm[:], 0.0)
+        nc.scalar.activation(out=warm[:], in_=warm[:], func=ACT.Gelu_apprx_tanh)
+        make_identity(nc, ident_f[:])
+        make_identity(nc, ident_b[:])
+        nc.gpsimd.memset(vec[:], 0.0)
+        load_z1(1, 0)
+        load_z1(1, 1)
+        nc.sync.dma_start(out=vec[0:1, :], in_=ln_scale.rearrange("(o d) -> o d", o=1))
+        nc.sync.dma_start(out=vec[1:2, :], in_=ln_offset.rearrange("(o d) -> o d", o=1))
+        nc.sync.dma_start(out=mean_sb[:], in_=mean_v)
+        nc.sync.dma_start(out=rstd_sb[:], in_=rstd_v)
+        load_w2(1)
+        nc.sync.dma_start(out=x_sb[:], in_=x_v)
+        load_w1(0)
+
+        gg = [grp(), grp()]
+
+        def tg(k, tpair, eng):
+            srcs = [g_sb[:, 2 * tpair + i, 512 * k : 512 * (k + 1)] for i in range(2)]
+            transposes(eng, srcs, gg[k], 256 * tpair)
+
+        sq(0, 0)
+        tg(0, 0, "v")
+        tg(1, 0, "v")
+        qq(0, 0)
+        ge(0, 0)
+        tg(0, 1, "s")
+        tg(1, 1, "v")
+        th(0, 0)
+        sq(0, 1)
+        xx(0, 0)
+        quant(gq[:, 0, :], gs[:, 0, :], gg[0], E5M2)
+        t2(0, 0, "s")
+        t2(0, 1, "v")
+        qq(0, 1)
+        quant(gq[:, 1, :], gs[:, 1, :], gg[1], E5M2)
+        t2(0, 2, "s")
+        t2(0, 3, "v")
+        ge(0, 1)
+        qw2(0, 0)
+        th(0, 1)
+        xx(0, 1)
+        qw2(0, 1)
+        sq(1, 0)
+        sq(1, 1)
+        for t in range(3):
+            dh(0, t)
+        for r, dst in ((0, sc), (1, off)):
+            for h in range(2):
+                bk = dw_bank()
+                nc.tensor.matmul(
+                    bk[:], lhsT=ident_b[:, r : r + 1].to_broadcast([P, P]), rhs=vec[:, 512 * h : 512 * (h + 1)],
+                    start=True, stop=True,
+                )
+                nc.scalar.copy(out=dst[:, 512 * h : 512 * (h + 1)], in_=bk[:])
+        nc.vector.tensor_scalar(out=nmean[:], in0=mean_sb[:], scalar1=-1.0, scalar2=None, op0=MUL)
+        nc.vector.tensor_scalar(out=k1[:], in0=rstd_sb[:], scalar1=1.0 / D, scalar2=None, op0=MUL)
+        nc.vector.tensor_tensor(out=r2[:], in0=rstd_sb[:], in1=rstd_sb[:], op=MUL)
+        nc.vector.tensor_tensor(out=k3[:], in0=r2[:], in1=k1[:], op=MUL)
+        dh(0, 3)
+
+        for c in range(NCH):
+            n = c + 1
+            more = n < NCH
+            more2 = c + 2 < NCH
+            old = c - LAG
+            if more2:
+                load_z1(c + 2, 0)
+                load_z1(c + 2, 1)
+                load_w2(c + 2)
+            if more:
+                load_w1(n)
+                t2(n, 0, "s")
+            hh(c, 0)
+            hh(c, 1)
+            if more:
+                qq(n, 0)
+                ge(n, 0)
+            dz(c, 0)
+            if more:
+                t2(n, 1, "s")
+            hh(c, 2)
+            hh(c, 3)
+            if more:
+                qq(n, 1)
+                th(n, 0)
+            dz(c, 1)
+            if more:
+                t2(n, 2, "s")
+                t2(n, 3, "s")
+                ge(n, 1)
+                xx(n, 0)
+            t3(c, 0, "s")
+            if more:
+                qw2(n, 0)
+                th(n, 1)
+            t3(c, 1, "s")
+            il(c)
+            if more:
+                xx(n, 1)
+                qw2(n, 1)
+                for t in range(3):
+                    dh(n, t)
+            if c < 2:
+                xn_elem(c)
+            qdz(c)
+            if old >= 0:
+                for m in range(4):
+                    dw(old, m, "s")
+            qdt(c)
+            if c < 2:
+                xn_il(c)
+            t1(c, 0, "s")
+            t1(c, 1, "s")
+            if old >= 0:
+                for m in range(4, 8):
+                    dw(old, m, "s")
+            t1(c, 2, "s")
+            qw1(c, 0)
+            t1(c, 3, "s")
+            if more2:
+                sq(c + 2, 0)
+                sq(c + 2, 1)
+            if c < 2:
+                xn_q(c)
+            qw1(c, 1)
+            if more:
+                dh(n, 3)
+
+        for t in range(4):
+            dxn(t, 0, 0, NCH)
+            dxn(t, 1, 0, NCH)
+            ep_a(t, 0)
+            ep_a(t, 1)
+            if t > 0:
+                ep_c(t - 1)
+            ep_b(t)
+            for m in range(4):
+                cm = 4 * t + m
+                dw(NCH - 2 + cm // 8, cm % 8, "s")
+            if t > 0:
+                ep_d(t - 1)
+        ep_c(3)
+        ep_d(3)

@@ -3,9 +3,9 @@ from contextlib import ExitStack
 import concourse.mybir as mybir
 from concourse.masks import make_identity
 
-S, D, F = 512, 1024, 3072
-FLOPS = 3 * 2 * S * D * F
-BYTES = 2 * (2 * S * D + 2 * D * F) + 4 * (S * F + S * D + D * F)
+TOKENS, D, HIDDEN = 512, 1024, 3072
+FLOPS = 3 * 2 * TOKENS * D * HIDDEN
+BYTES = 2 * (2 * TOKENS * D + 2 * D * HIDDEN) + 4 * (TOKENS * HIDDEN + TOKENS * D + D * HIDDEN)
 
 F32 = mybir.dt.float32
 BF16 = mybir.dt.bfloat16
@@ -19,42 +19,48 @@ MUL = mybir.AluOpType.mult
 ACT = mybir.ActivationFunctionType
 
 P = 128
-FC = 512
-NCH = F // FC
-LAG = 2
+CHUNK = 512
+CHUNKS = HIDDEN // CHUNK
+TILES = TOKENS // P
 
-A = 0.044715
-C = math_c = (2.0 / 3.141592653589793) ** 0.5
-BETA = 3.0 * A * C
-SQ_SCALE = BETA**0.5
+GELU_A = 0.044715
+GELU_C = 0.7978845608028654
+SQUARE_FACTOR = 3.0 * GELU_A * GELU_C
+
+W1_BLOCKS = (7, 9, 3, 1, 2, 2)
+W1_QUANTISED = (3, 4, 2, 0, 0, 2)
+OUT1_BLOCKS = (0, 0, 10, 7, 7, 5)
+XN_ITEMS = (8, 10, 0, 0, 0, 0)
+XN_GROUPED = (0, 2, 0, 0, 0, 0)
 
 
 def tile_transformerlayershard_pb_v_kernel(
     tc, x, attn_vec, ln_scale, ln_offset, wo, w1, b1, w2, b2, z1, mean, rstd, grad_out, out_0, out_1
 ):
     nc = tc.nc
-    x_v = x[0].rearrange("(p j) d -> p j d", j=4)
-    g_v = grad_out[0].rearrange("(p j) d -> p j d", j=4)
-    z1_v = z1[0].rearrange("(p j) f -> p j f", j=4)
-    mean_v = mean[0].rearrange("(p j) o -> p (j o)", j=4)
-    rstd_v = rstd[0].rearrange("(p j) o -> p (j o)", j=4)
-    w1_v = w1.rearrange("(m p) f -> p m f", p=P)
-    w2_v = w2.rearrange("(m p) d -> p m d", p=P)
-    o0_v = out_0[0].rearrange("(p j) d -> p j d", j=4)
-    o1_v = out_1.rearrange("(m p) f -> p m f", p=P)
+    x_hbm = x[0].rearrange("(p j) d -> p j d", j=TILES)
+    grad_hbm = grad_out[0].rearrange("(p j) d -> p j d", j=TILES)
+    z1_hbm = z1[0].rearrange("(p j) f -> p j f", j=TILES)
+    mean_hbm = mean[0].rearrange("(p j) o -> p (j o)", j=TILES)
+    rstd_hbm = rstd[0].rearrange("(p j) o -> p (j o)", j=TILES)
+    out0_hbm = out_0[0].rearrange("(p j) d -> p j d", j=TILES)
+    w1_hbm = w1.rearrange("(m p) f -> p m f", p=P)
+    w2_hbm = w2.rearrange("(m p) d -> p m d", p=P)
+    out1_hbm = out_1.rearrange("(m p) f -> p m f", p=P)
 
     with ExitStack() as ctx:
-        sb = ctx.enter_context(tc.tile_pool(name="sb", bufs=1))
-        ps = ctx.enter_context(tc.psum_pool(name="ps", bufs=1))
+        sbuf = ctx.enter_context(tc.tile_pool(name="sbuf", bufs=1))
+        psum = ctx.enter_context(tc.psum_pool(name="psum", bufs=1))
+        ctx.enter_context(tc.manual_schedule())
 
-        def st(shape, dtype, tag, bufs):
-            return sb.tile(shape, dtype, name=tag, tag=tag, bufs=bufs, align_bytes=64)
+        def tile(shape, dtype, tag, bufs):
+            return sbuf.tile(shape, dtype, name=tag, tag=tag, bufs=bufs, align_bytes=64)
 
         def bank(tag, bufs):
-            return ps.tile([P, 512], F32, name=tag, tag=tag, bufs=bufs)
+            return psum.tile([P, 512], F32, name=tag, tag=tag, bufs=bufs)
 
-        def tp_bank():
-            return bank("tp", 3)
+        def turn_bank():
+            return bank("turn", 3)
 
         def dh_bank():
             return bank("dh", 3)
@@ -62,457 +68,588 @@ def tile_transformerlayershard_pb_v_kernel(
         def dw_bank():
             return bank("dw", 2)
 
-        ident_f = st([P, P], F32, "ident_f", 1)
-        ident_b = st([P, P], BF16, "ident_b", 1)
-        vec = st([P, D], BF16, "vec", 1)
-        sc = st([P, D], BF16, "sc", 1)
-        off = st([P, D], BF16, "off", 1)
-        x_sb = st([P, 4, D], BF16, "x_sb", 1)
-        mean_sb = st([P, 4], F32, "mean_sb", 1)
-        rstd_sb = st([P, 4], F32, "rstd_sb", 1)
-        nmean = st([P, 4], F32, "nmean", 1)
-        k1 = st([P, 4], F32, "k1", 1)
-        r2 = st([P, 4], F32, "r2", 1)
-        k3 = st([P, 4], F32, "k3", 1)
-        warm = st([P, 1], F32, "warm", 1)
-        gq = st([P, 2, S], U32, "gq", 1)
-        gs = st([P, 2, S], U8, "gs", 1)
-        xnq = st([P, D], U32, "xnq", 1)
-        xns = st([P, D], U8, "xns", 1)
+        def once(made, key, make):
+            if key not in made:
+                made[key] = make()
+            return made[key]
 
-        z1t, w1t, w2t = {}, {}, {}
-        sqt, qt, get, xt = {}, {}, {}, {}
-        w2g, w2q, w2s = {}, {}, {}
-        w1g, w1q, w1s = {}, {}, {}
-        dht, ht, dzt, dzi = {}, {}, {}, {}
-        dzq, dzs, dtg, dtq, dts = {}, {}, {}, {}, {}
-        stage = {}
+        identity = tile([P, P], F32, "identity", 1)
+        scale_all = tile([P, D], BF16, "scale_all", 1)
+        offset_all = tile([P, D], BF16, "offset_all", 1)
+        x_sb = tile([P, TILES, D], BF16, "x_sb", 1)
+        mean_sb = tile([P, TILES], F32, "mean_sb", 1)
+        rstd_sb = tile([P, TILES], F32, "rstd_sb", 1)
+        neg_mean = tile([P, TILES], F32, "neg_mean", 1)
+        rstd_over_d = tile([P, TILES], F32, "rstd_over_d", 1)
+        rstd_squared = tile([P, TILES], F32, "rstd_squared", 1)
+        rstd_cubed_over_d = tile([P, TILES], F32, "rstd_cubed_over_d", 1)
+        table_load = tile([P, 1], F32, "table_load", 1)
+        grad_q = tile([P, 2, TOKENS], U32, "grad_q", 1)
+        grad_s = tile([P, 2, TOKENS], U8, "grad_s", 1)
+        xn_q = tile([P, D], U32, "xn_q", 1)
+        xn_s = tile([P, D], U8, "xn_s", 1)
+
+        z1_sb, w1_sb, w2_sb = {}, {}, {}
+        squares, tanhs, gelus, slopes = {}, {}, {}, {}
+        grad_grouped, w2_grouped, w2_q, w2_s = {}, {}, {}, {}
+        w1_grouped, w1_q, w1_s = {}, {}, {}
+        turned = {}
+        dh, gated, dz1 = {}, {}, {}
+        dz1_by_token, dz1_tok_q, dz1_tok_s = {}, {}, {}
+        dz1_by_hidden, dz1_hid_q, dz1_hid_s = {}, {}, {}
+        dw, dw_stage, dw_copied = {}, {}, {}
+        centred, xn, xn_by_token = {}, {}, {}
+        dxn, dx_scaled, dx_sums, dx_affine, dx_out = {}, {}, {}, {}, {}
 
         def load_z1(c, h):
-            t = st([P, 2, FC], F32, "z1t", 4)
-            nc.sync.dma_start(out=t[:], in_=z1_v[:, 2 * h : 2 * h + 2, c * FC : (c + 1) * FC])
-            z1t[c, h] = t
+            z1_sb[c, h] = tile([P, 2, CHUNK], F32, "z1_sb", 4)
+            nc.sync.dma_start(
+                out=z1_sb[c, h][:], in_=z1_hbm[:, 2 * h : 2 * h + 2, c * CHUNK : (c + 1) * CHUNK]
+            )
 
         def load_w2(c):
-            t = st([P, 4, D], BF16, "w2t", 2)
+            w2_sb[c] = tile([P, 4, D], BF16, "w2_sb", 2)
             for i in range(2):
                 nc.sync.dma_start(
-                    out=t[:, 2 * i : 2 * i + 2, :], in_=w2_v[:, 4 * c + 2 * i : 4 * c + 2 * i + 2, :]
+                    out=w2_sb[c][:, 2 * i : 2 * i + 2, :], in_=w2_hbm[:, 4 * c + 2 * i : 4 * c + 2 * i + 2, :]
                 )
-            w2t[c] = t
 
         def load_w1(c):
-            t = st([P, 8, FC], BF16, "w1t", 2)
-            nc.sync.dma_start(out=t[:], in_=w1_v[:, :, c * FC : (c + 1) * FC])
-            w1t[c] = t
+            w1_sb[c] = tile([P, 8, CHUNK], BF16, "w1_sb", 2)
+            nc.sync.dma_start(out=w1_sb[c][:], in_=w1_hbm[:, :, c * CHUNK : (c + 1) * CHUNK])
 
-        def sq(c, h):
-            t = st([P, 1024], F32, "sq", 2)
-            nc.scalar.activation(
-                out=t[:], in_=z1t[c, h][:].rearrange("p j f -> p (j f)"), func=ACT.Square, scale=SQ_SCALE
-            )
-            sqt[c, h] = t
+        def flat_z1(c, h):
+            return z1_sb[c, h][:].rearrange("p j f -> p (j f)")
 
-        def qq(c, h):
-            t = st([P, 1024], F32, "qt", 4)
+        def square(c, h):
+            squares[c, h] = tile([P, 1024], F32, "squares", 2)
+            nc.scalar.activation(out=squares[c, h][:], in_=flat_z1(c, h), func=ACT.Square, scale=SQUARE_FACTOR**0.5)
+
+        def cubic(c, h):
+            tanhs[c, h] = tile([P, 1024], F32, "tanhs", 4)
             nc.vector.scalar_tensor_tensor(
-                out=t[:], in0=sqt[c, h][:], scalar=BETA / A, in1=z1t[c, h][:].rearrange("p j f -> p (j f)"),
+                out=tanhs[c, h][:], in0=squares[c, h][:], scalar=SQUARE_FACTOR / GELU_A, in1=flat_z1(c, h),
                 op0=ADD, op1=MUL,
             )
-            qt[c, h] = t
 
-        def th(c, h):
-            t = qt[c, h]
-            nc.scalar.activation(out=t[:], in_=t[:], func=ACT.Tanh, scale=-A * C / BETA)
-
-        def ge(c, h):
-            t = st([P, 1024], F32, "ge", 2)
+        def tanh(c, h):
             nc.scalar.activation(
-                out=t[:], in_=z1t[c, h][:].rearrange("p j f -> p (j f)"), func=ACT.Gelu_apprx_tanh, scale=-1.0
+                out=tanhs[c, h][:], in_=tanhs[c, h][:], func=ACT.Tanh, scale=-GELU_A * GELU_C / SQUARE_FACTOR
             )
-            get[c, h] = t
 
-        def xx(c, h):
-            t = st([P, 1024], F32, "xt", 4)
+        def gelu(c, h):
+            gelus[c, h] = tile([P, 1024], F32, "gelus", 2)
+            nc.scalar.activation(out=gelus[c, h][:], in_=flat_z1(c, h), func=ACT.Gelu_apprx_tanh, scale=-1.0)
+
+        def slope(c, h):
+            slopes[c, h] = tile([P, 1024], F32, "slopes", 4)
             nc.vector.scalar_tensor_tensor(
-                out=t[:], in0=sqt[c, h][:], scalar=BETA / (3.0 * A), in1=get[c, h][:], op0=ADD, op1=MUL
+                out=slopes[c, h][:], in0=squares[c, h][:], scalar=SQUARE_FACTOR / (3.0 * GELU_A), in1=gelus[c, h][:],
+                op0=ADD, op1=MUL,
             )
-            xt[c, h] = t
 
-        def grp():
-            return st([P, 512, 4], BF16, "grp", 5)
-
-        def evac(eng, dst, r0, bk):
-            out = dst[:, r0 : r0 + 256, :].rearrange("p r j -> p (r j)").bitcast(F32)
-            out = out.rearrange("p (m r u) -> p m r u", m=2, u=2)
-            src = bk[:].rearrange("p (m u r) -> p m r u", m=2, u=2)
-            if eng == "v":
-                nc.vector.tensor_copy(out=out, in_=src)
-            else:
-                nc.scalar.copy(out=out, in_=src)
-
-        def transposes(eng, srcs, dst, r0):
-            bk = tp_bank()
+        def turn(key, blocks):
+            turned[key] = turn_bank()
             for i in range(2):
-                words = srcs[i].bitcast(F32)
+                words = blocks[i].bitcast(F32)
                 for u in range(2):
                     nc.tensor.transpose(
-                        bk[:, (2 * i + u) * P : (2 * i + u + 1) * P], words[:, u:256:2], ident_f[:]
+                        turned[key][:, (2 * i + u) * P : (2 * i + u + 1) * P], words[:, u:256:2], identity[:]
                     )
-            evac(eng, dst, r0, bk)
 
-        def quant(codes, scales, g, fmt):
-            nc.vector.quantize_mx(
-                out=codes.bitcast(fmt), scales=scales, in_=g[:].rearrange("p r j -> p (r j)")
+        def copy_turned(engine_copy, key, grouped, column):
+            words = grouped[:, column : column + 256, :].rearrange("p r j -> p (r j)").bitcast(F32)
+            engine_copy(
+                out=words.rearrange("p (i r u) -> p i r u", i=2, u=2),
+                in_=turned[key][:].rearrange("p (i u r) -> p i r u", i=2, u=2),
             )
 
-        def t2(c, b, eng):
-            k, mp = divmod(b, 2)
-            if mp == 0:
-                w2g[c, k] = grp()
-            if b == 0:
-                w2q[c] = st([P, 2, FC], U32, "w2q", 2)
-                w2s[c] = st([P, 2, FC], U8, "w2s", 2)
-            srcs = [w2t[c][:, 2 * mp + i, 512 * k : 512 * (k + 1)] for i in range(2)]
-            transposes(eng, srcs, w2g[c, k], 256 * mp)
+        def grouped_tile(tag, bufs):
+            return tile([P, 512, 4], BF16, tag, bufs)
 
-        def qw2(c, k):
-            quant(w2q[c][:, k, :], w2s[c][:, k, :], w2g[c, k], E4M3)
+        def quantise(codes, scales, grouped, fmt):
+            nc.vector.quantize_mx(
+                out=codes.bitcast(fmt), scales=scales, in_=grouped[:].rearrange("p r j -> p (r j)")
+            )
 
-        def t1(c, b, eng):
-            h, mp = divmod(b, 2)
-            if mp == 0:
-                w1g[c, h] = grp()
-            if b == 0:
-                w1q[c] = st([P, D], U32, "w1q", NCH)
-                w1s[c] = st([P, D], U8, "w1s", NCH)
-            srcs = [w1t[c][:, 4 * h + 2 * mp + i, :] for i in range(2)]
-            transposes(eng, srcs, w1g[c, h], 256 * mp)
+        def turn_grad(k, h):
+            turn(("grad", k, h), [grad_sb[:, 2 * h + i, 512 * k : 512 * (k + 1)] for i in range(2)])
 
-        def qw1(c, h):
-            cols = slice(512 * h, 512 * (h + 1))
-            quant(w1q[c][:, cols], w1s[c][:, cols], w1g[c, h], E4M3)
+        def copy_grad(k, h, engine_copy):
+            grouped = once(grad_grouped, k, lambda: grouped_tile("w2_grouped", 2))
+            copy_turned(engine_copy, ("grad", k, h), grouped, 256 * h)
 
-        def dh(c, t):
-            bk = dh_bank()
+        def quantise_grad(k):
+            quantise(grad_q[:, k, :], grad_s[:, k, :], grad_grouped[k], E5M2)
+
+        def turn_w2(c, b):
+            k, h = divmod(b, 2)
+            turn(("w2", c, b), [w2_sb[c][:, 2 * h + i, 512 * k : 512 * (k + 1)] for i in range(2)])
+
+        def copy_w2(c, b):
+            k, h = divmod(b, 2)
+            grouped = once(w2_grouped, (c, k), lambda: grouped_tile("w2_grouped", 2))
+            copy_turned(nc.scalar.copy, ("w2", c, b), grouped, 256 * h)
+
+        def quantise_w2(c, k):
+            codes = once(w2_q, c, lambda: tile([P, 2, CHUNK], U32, "w2_q", 2))
+            scales = once(w2_s, c, lambda: tile([P, 2, CHUNK], U8, "w2_s", 2))
+            quantise(codes[:, k, :], scales[:, k, :], w2_grouped[c, k], E4M3)
+
+        def turn_w1(c, b):
+            turn(("w1", c, b), [w1_sb[c][:, 2 * b + i, :] for i in range(2)])
+
+        def copy_w1(c, b):
+            grouped = once(w1_grouped, (c, b // 2), lambda: grouped_tile("w1_grouped", 2))
+            copy_turned(nc.scalar.copy, ("w1", c, b), grouped, 256 * (b % 2))
+
+        def quantise_w1(c, h):
+            codes = once(w1_q, c, lambda: tile([P, D], U32, "w1_q", CHUNKS))
+            scales = once(w1_s, c, lambda: tile([P, D], U8, "w1_s", CHUNKS))
+            columns = slice(512 * h, 512 * (h + 1))
+            quantise(codes[:, columns], scales[:, columns], w1_grouped[c, h], E4M3)
+
+        def multiply_dh(c, t):
+            dh[c, t] = dh_bank()
             for k in range(2):
                 nc.tensor.matmul_mx(
-                    out=bk[:],
-                    lhsT=gq[:, k, P * t : P * (t + 1)].bitcast(E5M2),
-                    lhsT_scale=gs[:, k, P * t : P * (t + 1)],
-                    rhs=w2q[c][:, k, :].bitcast(E4M3),
-                    rhs_scale=w2s[c][:, k, :],
+                    out=dh[c, t][:],
+                    lhsT=grad_q[:, k, P * t : P * (t + 1)].bitcast(E5M2),
+                    lhsT_scale=grad_s[:, k, P * t : P * (t + 1)],
+                    rhs=w2_q[c][:, k, :].bitcast(E4M3),
+                    rhs_scale=w2_s[c][:, k, :],
                     start=(k == 0),
                     stop=(k == 1),
                 )
-            dht[c, t] = bk
 
-        def hh(c, t):
+        def gate(c, t):
             h, i = divmod(t, 2)
-            if i == 0:
-                ht[c, h] = st([P, 1024], F32, "hh", 2)
-            cols = slice(512 * i, 512 * (i + 1))
+            out = once(gated, (c, h), lambda: tile([P, 1024], F32, "gated", 2))
+            columns = slice(512 * i, 512 * (i + 1))
             nc.vector.scalar_tensor_tensor(
-                out=ht[c, h][:, cols], in0=qt[c, h][:, cols], scalar=-1.0, in1=dht[c, t][:], op0=ADD, op1=MUL
+                out=out[:, columns], in0=tanhs[c, h][:, columns], scalar=-1.0, in1=dh[c, t][:], op0=ADD, op1=MUL
             )
 
-        def dz(c, h):
-            if h == 0:
-                dzt[c] = st([P, 4, FC], BF16, "dz", 2)
+        def make_dz1(c, h):
+            out = once(dz1, c, lambda: tile([P, TILES, CHUNK], BF16, "dz1", 2))
             nc.vector.scalar_tensor_tensor(
-                out=dzt[c][:, 2 * h : 2 * h + 2, :].rearrange("p j f -> p (j f)"),
-                in0=xt[c, h][:], scalar=-0.5, in1=ht[c, h][:], op0=ADD, op1=MUL,
+                out=out[:, 2 * h : 2 * h + 2, :].rearrange("p j f -> p (j f)"),
+                in0=slopes[c, h][:], scalar=-0.5, in1=gated[c, h][:], op0=ADD, op1=MUL,
             )
 
-        def interleave(src):
-            g = grp()
-            nc.vector.tensor_copy(out=g[:], in_=src[:].rearrange("p j f -> p f j"))
-            return g
+        def group_tokens(engine_copy, grouped, tiles):
+            engine_copy(
+                out=grouped[:].rearrange("p (r i) j -> p r j i", i=4),
+                in_=tiles[:].rearrange("p j (r i) -> p r j i", i=4),
+            )
 
-        def il(c):
-            dzi[c] = interleave(dzt[c])
+        def group_dz1(c):
+            dz1_by_token[c] = grouped_tile("dz1_by_token", 1)
+            group_tokens(nc.vector.tensor_copy, dz1_by_token[c], dz1[c])
 
-        def qdz(c):
-            dzq[c] = st([P, FC], U32, "dzq", 3)
-            dzs[c] = st([P, FC], U8, "dzs", 3)
-            quant(dzq[c][:], dzs[c][:], dzi[c], E5M2)
+        def quantise_dz1_tokens(c):
+            dz1_tok_q[c] = tile([P, CHUNK], U32, "dz1_tok_q", 3)
+            dz1_tok_s[c] = tile([P, CHUNK], U8, "dz1_tok_s", 3)
+            quantise(dz1_tok_q[c][:], dz1_tok_s[c][:], dz1_by_token[c], E5M2)
 
-        def t3(c, b, eng):
-            if b == 0:
-                dtg[c] = grp()
-            srcs = [dzt[c][:, 2 * b + i, :] for i in range(2)]
-            transposes(eng, srcs, dtg[c], 256 * b)
+        def turn_dz1(c, h):
+            turn(("dz1", c, h), [dz1[c][:, 2 * h + i, :] for i in range(2)])
 
-        def qdt(c):
-            dtq[c] = st([P, S], U32, "dtq", NCH)
-            dts[c] = st([P, S], U8, "dts", NCH)
-            quant(dtq[c][:], dts[c][:], dtg[c], E5M2)
+        def copy_dz1(c, h):
+            grouped = once(dz1_by_hidden, c, lambda: grouped_tile("dz1_by_hidden", 1))
+            copy_turned(nc.scalar.copy, ("dz1", c, h), grouped, 256 * h)
 
-        def dw(c, m, eng):
-            bk = dw_bank()
+        def quantise_dz1_hidden(c):
+            dz1_hid_q[c] = tile([P, TOKENS], U32, "dz1_hid_q", CHUNKS)
+            dz1_hid_s[c] = tile([P, TOKENS], U8, "dz1_hid_s", CHUNKS)
+            quantise(dz1_hid_q[c][:], dz1_hid_s[c][:], dz1_by_hidden[c], E5M2)
+
+        def centre(h, t):
+            out = once(centred, (h, t // 2), lambda: tile([P, 1024], F32, "gated", 2))
+            features = slice(512 * h, 512 * (h + 1))
+            nc.vector.scalar_tensor_tensor(
+                out=out[:, 512 * (t % 2) : 512 * (t % 2 + 1)], in0=x_sb[:, t, features],
+                scalar=mean_sb[:, t : t + 1], in1=scale_all[:, features], op0=SUB, op1=MUL,
+            )
+
+        def normalise(h, t):
+            out = once(xn, h, lambda: tile([P, TILES, 512], BF16, "stage", 4))
+            nc.vector.scalar_tensor_tensor(
+                out=out[:, t, :], in0=centred[h, t // 2][:, 512 * (t % 2) : 512 * (t % 2 + 1)],
+                scalar=rstd_sb[:, t : t + 1], in1=offset_all[:, 512 * h : 512 * (h + 1)], op0=MUL, op1=ADD,
+            )
+
+        def group_xn(h):
+            xn_by_token[h] = grouped_tile("stage", 4)
+            group_tokens(nc.scalar.copy, xn_by_token[h], xn[h])
+
+        def quantise_xn(h):
+            features = slice(512 * h, 512 * (h + 1))
+            quantise(xn_q[:, features], xn_s[:, features], xn_by_token[h], E4M3)
+
+        def multiply_dw(c, m):
+            dw[c, m] = dw_bank()
             nc.tensor.matmul_mx(
-                out=bk[:],
-                lhsT=xnq[:, P * m : P * (m + 1)].bitcast(E4M3),
-                lhsT_scale=xns[:, P * m : P * (m + 1)],
-                rhs=dzq[c][:].bitcast(E5M2),
-                rhs_scale=dzs[c][:],
+                out=dw[c, m][:],
+                lhsT=xn_q[:, P * m : P * (m + 1)].bitcast(E4M3),
+                lhsT_scale=xn_s[:, P * m : P * (m + 1)],
+                rhs=dz1_tok_q[c][:].bitcast(E5M2),
+                rhs_scale=dz1_tok_s[c][:],
                 start=True,
                 stop=True,
             )
-            if m % 2 == 0:
-                stage[c, m] = st([P, 2, FC], F32, "stage", 3)
-            t = stage[c, m - m % 2]
-            if eng == "v":
-                nc.vector.tensor_copy(out=t[:, m % 2, :], in_=bk[:])
-            else:
-                nc.scalar.copy(out=t[:, m % 2, :], in_=bk[:])
+
+        def copy_dw(c, m):
+            pair = m // 2
+            out = once(dw_stage, (c, pair), lambda: tile([P, 2, CHUNK], F32, "stage", 4))
+            nc.scalar.copy(out=out[:, m % 2, :], in_=dw[c, m][:])
             if m % 2 == 1:
-                nc.sync.dma_start(out=o1_v[:, m - 1 : m + 1, c * FC : (c + 1) * FC], in_=t[:])
-
-        xna = {}
-
-        def xn_a(h, t):
-            if t % 2 == 0:
-                xna[h, t // 2] = st([P, 1024], F32, "hh", 2)
-            a = xna[h, t // 2]
-            nc.vector.scalar_tensor_tensor(
-                out=a[:, 512 * (t % 2) : 512 * (t % 2 + 1)], in0=x_sb[:, t, 512 * h : 512 * (h + 1)],
-                scalar=mean_sb[:, t : t + 1], in1=sc[:, 512 * h : 512 * (h + 1)], op0=SUB, op1=MUL,
-            )
-
-        xnb = {}
-
-        def xn_b(h, t):
-            if t == 0:
-                xnb[h] = st([P, 4, 512], BF16, "xn", 1)
-            a = xna[h, t // 2]
-            nc.vector.scalar_tensor_tensor(
-                out=xnb[h][:, t, :], in0=a[:, 512 * (t % 2) : 512 * (t % 2 + 1)],
-                scalar=rstd_sb[:, t : t + 1], in1=off[:, 512 * h : 512 * (h + 1)], op0=MUL, op1=ADD,
-            )
-
-        def xn_elem(h):
-            xn_a(h, 0)
-            xn_a(h, 1)
-            xn_b(h, 0)
-            xn_a(h, 2)
-            xn_b(h, 1)
-            xn_a(h, 3)
-            xn_b(h, 2)
-            xn_b(h, 3)
-
-        xni = {}
-
-        def xn_il(h):
-            xni[h] = interleave(xnb[h])
-
-        def xn_q(h):
-            cols = slice(512 * h, 512 * (h + 1))
-            quant(xnq[:, cols], xns[:, cols], xni[h], E4M3)
-
-        dxt = {}
-
-        def dxn(t, h, c0, c1):
-            if c0 == 0:
-                dxt[t, h] = dh_bank() if h == 0 else tp_bank()
-            for c in range(c0, c1):
-                nc.tensor.matmul_mx(
-                    out=dxt[t, h][:],
-                    lhsT=dtq[c][:, P * t : P * (t + 1)].bitcast(E5M2),
-                    lhsT_scale=dts[c][:, P * t : P * (t + 1)],
-                    rhs=w1q[c][:, 512 * h : 512 * (h + 1)].bitcast(E4M3),
-                    rhs_scale=w1s[c][:, 512 * h : 512 * (h + 1)],
-                    start=(c == 0),
-                    stop=(c == NCH - 1),
+                nc.sync.dma_start(
+                    out=out1_hbm[:, 2 * pair : 2 * pair + 2, c * CHUNK : (c + 1) * CHUNK], in_=out[:]
                 )
 
-        at, tmpt, sums = {}, {}, {}
+        def multiply_dxn(t, h, first, last):
+            group = 2 * t + h
+            out = once(dxn, (t, h), lambda: turn_bank() if 3 <= group < 6 else dh_bank())
+            for c in range(first, last):
+                nc.tensor.matmul_mx(
+                    out=out[:],
+                    lhsT=dz1_hid_q[c][:, P * t : P * (t + 1)].bitcast(E5M2),
+                    lhsT_scale=dz1_hid_s[c][:, P * t : P * (t + 1)],
+                    rhs=w1_q[c][:, 512 * h : 512 * (h + 1)].bitcast(E4M3),
+                    rhs_scale=w1_s[c][:, 512 * h : 512 * (h + 1)],
+                    start=(c == 0),
+                    stop=(c == CHUNKS - 1),
+                )
 
-        def ep_a(t, h):
-            if h == 0:
-                at[t] = st([P, D], F32, "qt", 4)
-                sums[t] = st([P, 8], F32, "sums", 4)
-            cols = slice(512 * h, 512 * (h + 1))
+        def scale_dxn(t, h):
+            out = once(dx_scaled, t, lambda: tile([P, D], F32, "tanhs", 4))
+            sums = once(dx_sums, t, lambda: tile([P, 8], F32, "dx_sums", 4))
+            features = slice(512 * h, 512 * (h + 1))
             nc.vector.scalar_tensor_tensor(
-                out=at[t][:, cols], in0=dxt[t, h][:], scalar=1.0, in1=sc[:, cols], op0=MUL, op1=MUL,
-                accum_out=sums[t][:, h : h + 1],
+                out=out[:, features], in0=dxn[t, h][:], scalar=1.0, in1=scale_all[:, features], op0=MUL, op1=MUL,
+                accum_out=sums[:, h : h + 1],
             )
 
-        def ep_b(t):
-            junk = st([P, D], F32, "sq", 2)
+        def dot_dxn(t):
+            products = tile([P, D], F32, "squares", 2)
             nc.vector.scalar_tensor_tensor(
-                out=junk[:], in0=x_sb[:, t, :], scalar=mean_sb[:, t : t + 1], in1=at[t][:], op0=SUB, op1=MUL,
-                accum_out=sums[t][:, 2:3],
+                out=products[:], in0=x_sb[:, t, :], scalar=mean_sb[:, t : t + 1], in1=dx_scaled[t][:],
+                op0=SUB, op1=MUL, accum_out=dx_sums[t][:, 2:3],
             )
 
-        def ep_c(t):
-            s = sums[t]
-            nc.vector.scalar_tensor_tensor(
-                out=s[:, 3:4], in0=s[:, 0:1], scalar=s[:, 1:2], in1=k1[:, t : t + 1], op0=ADD, op1=MUL
-            )
-            nc.vector.tensor_tensor(out=s[:, 4:5], in0=s[:, 2:3], in1=k3[:, t : t + 1], op=MUL)
-            nc.vector.scalar_tensor_tensor(
-                out=s[:, 5:6], in0=s[:, 4:5], scalar=nmean[:, t : t + 1], in1=s[:, 3:4], op0=MUL, op1=ADD
-            )
-            tmpt[t] = st([P, D], F32, "ge", 2)
+        def coefficients(t):
+            sums = dx_sums[t]
+            token = slice(t, t + 1)
+            second_half, slope_x, row_mean, offset_x = (sums[:, i : i + 1] for i in (3, 4, 6, 5))
+            identity_of = ACT.Identity
+            nc.scalar.activation(out=second_half, in_=sums[:, 1:2], func=identity_of, scale=rstd_over_d[:, token])
+            nc.scalar.activation(out=slope_x, in_=sums[:, 2:3], func=identity_of, scale=rstd_cubed_over_d[:, token])
             nc.scalar.activation(
-                out=tmpt[t][:], in_=x_sb[:, t, :], func=ACT.Identity, scale=s[:, 4:5], bias=s[:, 5:6]
+                out=row_mean, in_=sums[:, 0:1], func=identity_of, scale=rstd_over_d[:, token], bias=second_half
+            )
+            nc.scalar.activation(out=offset_x, in_=slope_x, func=identity_of, scale=neg_mean[:, token], bias=row_mean)
+
+        def affine_x(t, lo, hi):
+            out = once(dx_affine, t, lambda: tile([P, D], F32, "gelus", 2))
+            nc.scalar.activation(
+                out=out[:, lo:hi], in_=x_sb[:, t, lo:hi], func=ACT.Identity,
+                scale=dx_sums[t][:, 4:5], bias=dx_sums[t][:, 5:6],
             )
 
-        def ep_d(t):
-            o = st([P, D], F32, "xt", 4)
+        def finish_dx(t, lo, hi):
+            out = once(dx_out, t, lambda: tile([P, D], F32, "slopes", 4))
             nc.vector.scalar_tensor_tensor(
-                out=o[:], in0=at[t][:], scalar=rstd_sb[:, t : t + 1], in1=tmpt[t][:], op0=MUL, op1=SUB
+                out=out[:, lo:hi], in0=dx_scaled[t][:, lo:hi], scalar=rstd_sb[:, t : t + 1],
+                in1=dx_affine[t][:, lo:hi], op0=MUL, op1=SUB,
             )
-            nc.sync.dma_start(out=o0_v[:, t, :], in_=o[:])
+            nc.sync.dma_start(out=out0_hbm[:, t, lo:hi], in_=out[:, lo:hi])
+
+        w1_blocks = [(c, b) for c in range(CHUNKS) for b in range(4)]
+        dw_blocks = [(c, m) for c in range(CHUNKS) for m in range(8)]
+        queues = {
+            turn_w1: w1_blocks,
+            copy_w1: w1_blocks,
+            quantise_w1: [(c, h) for c in range(CHUNKS) for h in range(2)],
+            multiply_dw: dw_blocks,
+            copy_dw: dw_blocks,
+            group_xn: [(0,), (1,)],
+        }
+
+        def xn_work(piece, *args):
+            piece(*args)
+
+        queues[xn_work] = []
+        for h in range(2):
+            for piece, t in (
+                (centre, 0), (centre, 1), (normalise, 0), (centre, 2), (normalise, 1), (centre, 3), (normalise, 2),
+                (normalise, 3),
+            ):
+                queues[xn_work].append((piece, h, t))
+            queues[xn_work].append((quantise_xn, h))
+        share = {
+            turn_w1: W1_BLOCKS,
+            copy_w1: W1_BLOCKS,
+            quantise_w1: W1_QUANTISED,
+            multiply_dw: OUT1_BLOCKS,
+            copy_dw: OUT1_BLOCKS,
+            xn_work: XN_ITEMS,
+            group_xn: XN_GROUPED,
+        }
+        begun = {}
+
+        def run_next(work):
+            i = begun.get(work, 0)
+            begun[work] = i + 1
+            work(*queues[work][i])
+
+        def take(c, work, slot):
+            if slot < share[work][c]:
+                run_next(work)
+
+        def at(work, c, *args):
+            if 0 <= c < CHUNKS:
+                work(c, *args)
 
         load_z1(0, 0)
-        g_sb = st([P, 4, D], BF16, "w2t", 2)
+        grad_sb = tile([P, TILES, D], BF16, "w2_sb", 2)
         for i in range(2):
-            nc.sync.dma_start(out=g_sb[:, 2 * i : 2 * i + 2, :], in_=g_v[:, 2 * i : 2 * i + 2, :])
+            nc.sync.dma_start(out=grad_sb[:, 2 * i : 2 * i + 2, :], in_=grad_hbm[:, 2 * i : 2 * i + 2, :])
         load_z1(0, 1)
         load_w2(0)
-        nc.vector.memset(warm[:], 0.0)
-        nc.scalar.activation(out=warm[:], in_=warm[:], func=ACT.Gelu_apprx_tanh)
-        make_identity(nc, ident_f[:])
-        make_identity(nc, ident_b[:])
-        nc.gpsimd.memset(vec[:], 0.0)
+        nc.vector.memset(table_load[:], 0.0)
+        nc.scalar.activation(out=table_load[:], in_=table_load[:], func=ACT.Gelu_apprx_tanh)
+        make_identity(nc, identity[:])
+        nc.sync.dma_start(out=mean_sb[:], in_=mean_hbm)
+        nc.sync.dma_start(out=rstd_sb[:], in_=rstd_hbm)
+        nc.gpsimd.tensor_scalar(out=neg_mean[:], in0=mean_sb[:], scalar1=-1.0, scalar2=0.0, op0=MUL, op1=ADD)
+        nc.gpsimd.tensor_scalar(out=rstd_over_d[:], in0=rstd_sb[:], scalar1=1.0 / D, scalar2=0.0, op0=MUL, op1=ADD)
+        nc.gpsimd.tensor_tensor(out=rstd_squared[:], in0=rstd_sb[:], in1=rstd_sb[:], op=MUL)
+        nc.gpsimd.tensor_tensor(out=rstd_cubed_over_d[:], in0=rstd_squared[:], in1=rstd_over_d[:], op=MUL)
         load_z1(1, 0)
         load_z1(1, 1)
-        nc.sync.dma_start(out=vec[0:1, :], in_=ln_scale.rearrange("(o d) -> o d", o=1))
-        nc.sync.dma_start(out=vec[1:2, :], in_=ln_offset.rearrange("(o d) -> o d", o=1))
-        nc.sync.dma_start(out=mean_sb[:], in_=mean_v)
-        nc.sync.dma_start(out=rstd_sb[:], in_=rstd_v)
         load_w2(1)
-        nc.sync.dma_start(out=x_sb[:], in_=x_v)
         load_w1(0)
+        nc.sync.dma_start(out=x_sb[:], in_=x_hbm)
+        nc.sync.dma_start(out=scale_all[:], in_=ln_scale.partition_broadcast(P))
+        nc.sync.dma_start(out=offset_all[:], in_=ln_offset.partition_broadcast(P))
+        load_w1(1)
+        square(0, 0)
+        gelu(0, 0)
+        turn_grad(0, 0)
+        cubic(0, 0)
+        turn_grad(1, 0)
+        copy_grad(0, 0, nc.scalar.copy)
+        turn_grad(1, 1)
+        slope(0, 0)
+        turn_grad(0, 1)
+        copy_grad(1, 1, nc.scalar.copy)
+        copy_grad(1, 0, nc.vector.tensor_copy)
+        gelu(0, 1)
+        copy_grad(0, 1, nc.vector.tensor_copy)
+        turn_w2(0, 2)
+        quantise_grad(1)
+        square(0, 1)
+        turn_w2(0, 0)
+        quantise_grad(0)
+        turn_w2(0, 3)
+        copy_w2(0, 2)
+        slope(0, 1)
+        copy_w2(0, 0)
+        turn_w2(0, 1)
+        copy_w2(0, 3)
+        cubic(0, 1)
+        copy_w2(0, 1)
+        square(1, 0)
+        quantise_w2(0, 0)
+        quantise_w2(0, 1)
+        multiply_dh(0, 2)
+        tanh(0, 1)
+        multiply_dh(0, 3)
+        square(1, 1)
+        turn_w2(1, 2)
+        tanh(0, 0)
+        gelu(1, 0)
 
-        gg = [grp(), grp()]
+        for c in range(CHUNKS):
+            for i in (0, 1):
+                at(load_z1, c + 2, i)
+            at(load_w2, c + 2)
+            at(load_w1, c + 2)
+            at(cubic, c + 1, 0)
+            at(multiply_dh, c, 1)
+            at(turn_w2, c + 1, 3)
+            for i in (2, 3):
+                at(gate, c, i)
+            at(cubic, c + 1, 1)
+            at(gelu, c + 1, 1)
+            at(turn_dz1, c - 1, 0)
+            at(copy_w2, c + 1, 2)
+            at(make_dz1, c, 1)
+            at(copy_w2, c + 1, 3)
+            for slot in (6, 4):
+                take(c, multiply_dw, slot)
+            for slot in (4, 2):
+                take(c, turn_w1, slot)
+            for i in (1, 0):
+                at(turn_w2, c + 1, i)
+            at(multiply_dh, c, 0)
+            take(c, copy_dw, 1)
+            at(copy_dz1, c - 1, 0)
+            take(c, copy_w1, 2)
+            take(c, group_xn, 1)
+            take(c, quantise_w1, 3)
+            at(group_dz1, c - 1)
+            take(c, copy_w1, 4)
+            at(slope, c + 1, 0)
+            for i in (1, 0):
+                at(copy_w2, c + 1, i)
+            at(slope, c + 1, 1)
+            at(quantise_w2, c + 1, 1)
+            for slot in (4, 2):
+                take(c, xn_work, slot)
+            take(c, multiply_dw, 0)
+            take(c, turn_w1, 5)
+            take(c, multiply_dw, 9)
+            for slot in (1, 0):
+                take(c, turn_w1, slot)
+            take(c, copy_dw, 0)
+            at(tanh, c + 1, 1)
+            take(c, copy_w1, 3)
+            take(c, quantise_w1, 0)
+            for slot in (1, 9, 6):
+                take(c, xn_work, slot)
+            at(quantise_w2, c + 1, 0)
+            take(c, xn_work, 5)
+            for slot in (1, 7):
+                take(c, multiply_dw, slot)
+            take(c, turn_w1, 3)
+            at(turn_dz1, c, 1)
+            take(c, turn_w1, 8)
+            take(c, multiply_dw, 8)
+            take(c, xn_work, 7)
+            at(quantise_dz1_hidden, c - 1)
+            take(c, turn_w1, 7)
+            take(c, copy_dw, 2)
+            take(c, copy_w1, 0)
+            take(c, xn_work, 3)
+            take(c, multiply_dw, 5)
+            take(c, xn_work, 0)
+            for i in (1, 0):
+                at(gate, c, i)
+            at(quantise_dz1_tokens, c - 1)
+            take(c, turn_w1, 6)
+            for i in (2, 3):
+                at(multiply_dh, c + 1, i)
+            at(turn_w2, c + 2, 2)
+            take(c, multiply_dw, 3)
+            take(c, copy_dw, 4)
+            take(c, multiply_dw, 2)
+            take(c, copy_dw, 3)
+            at(tanh, c + 1, 0)
+            for slot in (8, 9):
+                take(c, copy_dw, slot)
+            take(c, copy_w1, 5)
+            at(square, c + 2, 0)
+            take(c, copy_w1, 6)
+            take(c, quantise_w1, 2)
+            at(make_dz1, c, 0)
+            take(c, copy_dw, 6)
+            at(square, c + 2, 1)
+            at(gelu, c + 2, 0)
+            take(c, copy_dw, 5)
+            take(c, copy_w1, 1)
+            take(c, quantise_w1, 1)
+            at(copy_dz1, c, 1)
+            take(c, copy_dw, 7)
+            take(c, group_xn, 0)
+            take(c, copy_w1, 7)
+            take(c, xn_work, 8)
+            take(c, copy_w1, 8)
 
-        def tg(k, tpair, eng):
-            srcs = [g_sb[:, 2 * tpair + i, 512 * k : 512 * (k + 1)] for i in range(2)]
-            transposes(eng, srcs, gg[k], 256 * tpair)
-
-        sq(0, 0)
-        tg(0, 0, "v")
-        tg(1, 0, "v")
-        qq(0, 0)
-        ge(0, 0)
-        tg(0, 1, "s")
-        tg(1, 1, "v")
-        th(0, 0)
-        sq(0, 1)
-        xx(0, 0)
-        quant(gq[:, 0, :], gs[:, 0, :], gg[0], E5M2)
-        t2(0, 0, "s")
-        t2(0, 1, "v")
-        qq(0, 1)
-        quant(gq[:, 1, :], gs[:, 1, :], gg[1], E5M2)
-        t2(0, 2, "s")
-        t2(0, 3, "v")
-        ge(0, 1)
-        qw2(0, 0)
-        th(0, 1)
-        xx(0, 1)
-        qw2(0, 1)
-        sq(1, 0)
-        sq(1, 1)
-        for t in range(3):
-            dh(0, t)
-        for r, dst in ((0, sc), (1, off)):
-            for h in range(2):
-                bk = dw_bank()
-                nc.tensor.matmul(
-                    bk[:], lhsT=ident_b[:, r : r + 1].to_broadcast([P, P]), rhs=vec[:, 512 * h : 512 * (h + 1)],
-                    start=True, stop=True,
-                )
-                nc.scalar.copy(out=dst[:, 512 * h : 512 * (h + 1)], in_=bk[:])
-        nc.vector.tensor_scalar(out=nmean[:], in0=mean_sb[:], scalar1=-1.0, scalar2=None, op0=MUL)
-        nc.vector.tensor_scalar(out=k1[:], in0=rstd_sb[:], scalar1=1.0 / D, scalar2=None, op0=MUL)
-        nc.vector.tensor_tensor(out=r2[:], in0=rstd_sb[:], in1=rstd_sb[:], op=MUL)
-        nc.vector.tensor_tensor(out=k3[:], in0=r2[:], in1=k1[:], op=MUL)
-        dh(0, 3)
-
-        for c in range(NCH):
-            n = c + 1
-            more = n < NCH
-            more2 = c + 2 < NCH
-            old = c - LAG
-            if more2:
-                load_z1(c + 2, 0)
-                load_z1(c + 2, 1)
-                load_w2(c + 2)
-            if more:
-                load_w1(n)
-                t2(n, 0, "s")
-            hh(c, 0)
-            hh(c, 1)
-            if more:
-                qq(n, 0)
-                ge(n, 0)
-            dz(c, 0)
-            if more:
-                t2(n, 1, "s")
-            hh(c, 2)
-            hh(c, 3)
-            if more:
-                qq(n, 1)
-                th(n, 0)
-            dz(c, 1)
-            if more:
-                t2(n, 2, "s")
-                t2(n, 3, "s")
-                ge(n, 1)
-                xx(n, 0)
-            t3(c, 0, "s")
-            if more:
-                qw2(n, 0)
-                th(n, 1)
-            t3(c, 1, "s")
-            il(c)
-            if more:
-                xx(n, 1)
-                qw2(n, 1)
-                for t in range(3):
-                    dh(n, t)
-            if c < 2:
-                xn_elem(c)
-            qdz(c)
-            if old >= 0:
-                for m in range(4):
-                    dw(old, m, "s")
-            qdt(c)
-            if c < 2:
-                xn_il(c)
-            t1(c, 0, "s")
-            t1(c, 1, "s")
-            if old >= 0:
-                for m in range(4, 8):
-                    dw(old, m, "s")
-            t1(c, 2, "s")
-            qw1(c, 0)
-            t1(c, 3, "s")
-            if more2:
-                sq(c + 2, 0)
-                sq(c + 2, 1)
-            if c < 2:
-                xn_q(c)
-            qw1(c, 1)
-            if more:
-                dh(n, 3)
-
-        for t in range(4):
-            dxn(t, 0, 0, NCH)
-            dxn(t, 1, 0, NCH)
-            ep_a(t, 0)
-            ep_a(t, 1)
-            if t > 0:
-                ep_c(t - 1)
-            ep_b(t)
-            for m in range(4):
-                cm = 4 * t + m
-                dw(NCH - 2 + cm // 8, cm % 8, "s")
-            if t > 0:
-                ep_d(t - 1)
-        ep_c(3)
-        ep_d(3)
+        multiply_dxn(1, 0, 0, CHUNKS - 1)
+        for slot in range(2):
+            run_next(multiply_dw)
+        multiply_dxn(1, 1, 0, CHUNKS - 1)
+        run_next(copy_dw)
+        run_next(quantise_w1)
+        run_next(copy_dw)
+        group_dz1(5)
+        run_next(multiply_dw)
+        turn_dz1(5, 0)
+        run_next(copy_dw)
+        run_next(multiply_dw)
+        copy_dz1(5, 0)
+        run_next(multiply_dw)
+        multiply_dxn(0, 0, 0, CHUNKS - 1)
+        run_next(copy_dw)
+        quantise_dz1_hidden(5)
+        run_next(copy_dw)
+        quantise_dz1_tokens(5)
+        for slot in range(2):
+            run_next(multiply_dw)
+        run_next(copy_dw)
+        multiply_dxn(1, 0, CHUNKS - 1, CHUNKS)
+        multiply_dxn(0, 0, CHUNKS - 1, CHUNKS)
+        scale_dxn(1, 0)
+        run_next(copy_dw)
+        multiply_dxn(1, 1, CHUNKS - 1, CHUNKS)
+        run_next(multiply_dw)
+        scale_dxn(1, 1)
+        run_next(multiply_dw)
+        run_next(copy_dw)
+        multiply_dxn(3, 1, 0, CHUNKS - 1)
+        run_next(copy_dw)
+        dot_dxn(1)
+        run_next(multiply_dw)
+        scale_dxn(0, 0)
+        run_next(multiply_dw)
+        run_next(copy_dw)
+        multiply_dxn(3, 1, CHUNKS - 1, CHUNKS)
+        multiply_dxn(3, 0, 0, CHUNKS - 1)
+        scale_dxn(3, 1)
+        run_next(copy_dw)
+        coefficients(1)
+        multiply_dxn(3, 0, CHUNKS - 1, CHUNKS)
+        affine_x(1, 0, D)
+        run_next(multiply_dw)
+        scale_dxn(3, 0)
+        run_next(multiply_dw)
+        multiply_dxn(0, 1, 0, CHUNKS - 1)
+        run_next(copy_dw)
+        dot_dxn(3)
+        run_next(copy_dw)
+        multiply_dxn(0, 1, CHUNKS - 1, CHUNKS)
+        coefficients(3)
+        finish_dx(1, 0, D)
+        for slot in range(2):
+            run_next(multiply_dw)
+        run_next(copy_dw)
+        multiply_dxn(2, 0, 0, CHUNKS - 1)
+        affine_x(3, 0, D)
+        scale_dxn(0, 1)
+        run_next(copy_dw)
+        dot_dxn(0)
+        multiply_dxn(2, 0, CHUNKS - 1, CHUNKS)
+        for slot in range(2):
+            run_next(multiply_dw)
+        run_next(copy_dw)
+        multiply_dxn(2, 1, 0, CHUNKS - 1)
+        scale_dxn(2, 0)
+        coefficients(0)
+        finish_dx(3, 0, D)
+        run_next(copy_dw)
+        multiply_dxn(2, 1, CHUNKS - 1, CHUNKS)
+        affine_x(0, 0, D)
+        run_next(multiply_dw)
+        scale_dxn(2, 1)
+        run_next(multiply_dw)
+        dot_dxn(2)
+        for slot in range(2):
+            run_next(copy_dw)
+        coefficients(2)
+        finish_dx(0, 0, D)
+        affine_x(2, 0, 512)
+        affine_x(2, 512, D)
+        finish_dx(2, 0, 512)
+        finish_dx(2, 512, D)

from contextlib import ExitStack

import concourse.mybir as mybir
from concourse.masks import make_identity

TOKENS, D, HIDDEN = 512, 1024, 3072
FLOPS = 3 * 2 * TOKENS * D * HIDDEN
BYTES = 2 * (2 * TOKENS * D + 2 * D * HIDDEN) + 4 * (TOKENS * HIDDEN + TOKENS * D + D * HIDDEN)

F32 = mybir.dt.float32
BF16 = mybir.dt.bfloat16
U32 = mybir.dt.uint32
U8 = mybir.dt.uint8
E4M3 = mybir.dt.float8_e4m3fn_x4
E5M2 = mybir.dt.float8_e5m2_x4
ADD = mybir.AluOpType.add
SUB = mybir.AluOpType.subtract
MUL = mybir.AluOpType.mult
ACT = mybir.ActivationFunctionType

P = 128
CHUNK = 512
CHUNKS = HIDDEN // CHUNK
TILES = TOKENS // P

GELU_A = 0.044715
GELU_C = 0.7978845608028654
SQUARE_FACTOR = 3.0 * GELU_A * GELU_C

W1_BLOCKS = (7, 9, 3, 1, 2, 2)
W1_QUANTISED = (3, 4, 2, 0, 0, 2)
OUT1_BLOCKS = (0, 0, 10, 7, 7, 5)
XN_ITEMS = (8, 10, 0, 0, 0, 0)
XN_GROUPED = (0, 2, 0, 0, 0, 0)


def tile_transformerlayershard_pb_v_kernel(
    tc, x, attn_vec, ln_scale, ln_offset, wo, w1, b1, w2, b2, z1, mean, rstd, grad_out, out_0, out_1
):
    nc = tc.nc
    x_hbm = x[0].rearrange("(p j) d -> p j d", j=TILES)
    grad_hbm = grad_out[0].rearrange("(p j) d -> p j d", j=TILES)
    z1_hbm = z1[0].rearrange("(p j) f -> p j f", j=TILES)
    mean_hbm = mean[0].rearrange("(p j) o -> p (j o)", j=TILES)
    rstd_hbm = rstd[0].rearrange("(p j) o -> p (j o)", j=TILES)
    out0_hbm = out_0[0].rearrange("(p j) d -> p j d", j=TILES)
    w1_hbm = w1.rearrange("(m p) f -> p m f", p=P)
    w2_hbm = w2.rearrange("(m p) d -> p m d", p=P)
    out1_hbm = out_1.rearrange("(m p) f -> p m f", p=P)

    with ExitStack() as ctx:
        sbuf = ctx.enter_context(tc.tile_pool(name="sbuf", bufs=1))
        psum = ctx.enter_context(tc.psum_pool(name="psum", bufs=1))
        ctx.enter_context(tc.manual_schedule())

        def tile(shape, dtype, tag, bufs):
            return sbuf.tile(shape, dtype, name=tag, tag=tag, bufs=bufs, align_bytes=64)

        def bank(tag, bufs):
            return psum.tile([P, 512], F32, name=tag, tag=tag, bufs=bufs)

        def turn_bank():
            return bank("turn", 3)

        def dh_bank():
            return bank("dh", 3)

        def dw_bank():
            return bank("dw", 2)

        def once(made, key, make):
            if key not in made:
                made[key] = make()
            return made[key]

        identity = tile([P, P], F32, "identity", 1)
        scale_all = tile([P, D], BF16, "scale_all", 1)
        offset_all = tile([P, D], BF16, "offset_all", 1)
        x_sb = tile([P, TILES, D], BF16, "x_sb", 1)
        mean_sb = tile([P, TILES], F32, "mean_sb", 1)
        rstd_sb = tile([P, TILES], F32, "rstd_sb", 1)
        neg_mean = tile([P, TILES], F32, "neg_mean", 1)
        rstd_over_d = tile([P, TILES], F32, "rstd_over_d", 1)
        rstd_squared = tile([P, TILES], F32, "rstd_squared", 1)
        rstd_cubed_over_d = tile([P, TILES], F32, "rstd_cubed_over_d", 1)
        table_load = tile([P, 1], F32, "table_load", 1)
        grad_q = tile([P, 2, TOKENS], U32, "grad_q", 1)
        grad_s = tile([P, 2, TOKENS], U8, "grad_s", 1)
        xn_q = tile([P, D], U32, "xn_q", 1)
        xn_s = tile([P, D], U8, "xn_s", 1)

        z1_sb, w1_sb, w2_sb = {}, {}, {}
        squares, tanhs, gelus, slopes = {}, {}, {}, {}
        grad_grouped, w2_grouped, w2_q, w2_s = {}, {}, {}, {}
        w1_grouped, w1_q, w1_s = {}, {}, {}
        turned = {}
        dh, gated, dz1 = {}, {}, {}
        dz1_by_token, dz1_tok_q, dz1_tok_s = {}, {}, {}
        dz1_by_hidden, dz1_hid_q, dz1_hid_s = {}, {}, {}
        dw, dw_stage, dw_copied = {}, {}, {}
        centred, xn, xn_by_token = {}, {}, {}
        dxn, dx_scaled, dx_sums, dx_affine, dx_out = {}, {}, {}, {}, {}

        def load_z1(c, h):
            z1_sb[c, h] = tile([P, 2, CHUNK], F32, "z1_sb", 4)
            nc.sync.dma_start(
                out=z1_sb[c, h][:], in_=z1_hbm[:, 2 * h : 2 * h + 2, c * CHUNK : (c + 1) * CHUNK]
            )

        def load_w2(c):
            w2_sb[c] = tile([P, 4, D], BF16, "w2_sb", 2)
            for i in range(2):
                nc.sync.dma_start(
                    out=w2_sb[c][:, 2 * i : 2 * i + 2, :], in_=w2_hbm[:, 4 * c + 2 * i : 4 * c + 2 * i + 2, :]
                )

        def load_w1(c):
            w1_sb[c] = tile([P, 8, CHUNK], BF16, "w1_sb", 2)
            nc.sync.dma_start(out=w1_sb[c][:], in_=w1_hbm[:, :, c * CHUNK : (c + 1) * CHUNK])

        def flat_z1(c, h):
            return z1_sb[c, h][:].rearrange("p j f -> p (j f)")

        def square(c, h):
            squares[c, h] = tile([P, 1024], F32, "squares", 2)
            nc.scalar.activation(out=squares[c, h][:], in_=flat_z1(c, h), func=ACT.Square, scale=SQUARE_FACTOR**0.5)

        def cubic(c, h):
            tanhs[c, h] = tile([P, 1024], F32, "tanhs", 4)
            nc.vector.scalar_tensor_tensor(
                out=tanhs[c, h][:], in0=squares[c, h][:], scalar=SQUARE_FACTOR / GELU_A, in1=flat_z1(c, h),
                op0=ADD, op1=MUL,
            )

        def tanh(c, h):
            nc.scalar.activation(
                out=tanhs[c, h][:], in_=tanhs[c, h][:], func=ACT.Tanh, scale=-GELU_A * GELU_C / SQUARE_FACTOR
            )

        def gelu(c, h):
            gelus[c, h] = tile([P, 1024], F32, "gelus", 2)
            nc.scalar.activation(out=gelus[c, h][:], in_=flat_z1(c, h), func=ACT.Gelu_apprx_tanh, scale=-1.0)

        def slope(c, h):
            slopes[c, h] = tile([P, 1024], F32, "slopes", 4)
            nc.vector.scalar_tensor_tensor(
                out=slopes[c, h][:], in0=squares[c, h][:], scalar=SQUARE_FACTOR / (3.0 * GELU_A), in1=gelus[c, h][:],
                op0=ADD, op1=MUL,
            )

        def turn(key, blocks):
            turned[key] = turn_bank()
            for i in range(2):
                words = blocks[i].bitcast(F32)
                for u in range(2):
                    nc.tensor.transpose(
                        turned[key][:, (2 * i + u) * P : (2 * i + u + 1) * P], words[:, u:256:2], identity[:]
                    )

        def copy_turned(engine_copy, key, grouped, column):
            words = grouped[:, column : column + 256, :].rearrange("p r j -> p (r j)").bitcast(F32)
            engine_copy(
                out=words.rearrange("p (i r u) -> p i r u", i=2, u=2),
                in_=turned[key][:].rearrange("p (i u r) -> p i r u", i=2, u=2),
            )

        def grouped_tile(tag, bufs):
            return tile([P, 512, 4], BF16, tag, bufs)

        def quantise(codes, scales, grouped, fmt):
            nc.vector.quantize_mx(
                out=codes.bitcast(fmt), scales=scales, in_=grouped[:].rearrange("p r j -> p (r j)")
            )

        def turn_grad(k, h):
            turn(("grad", k, h), [grad_sb[:, 2 * h + i, 512 * k : 512 * (k + 1)] for i in range(2)])

        def copy_grad(k, h, engine_copy):
            grouped = once(grad_grouped, k, lambda: grouped_tile("w2_grouped", 2))
            copy_turned(engine_copy, ("grad", k, h), grouped, 256 * h)

        def quantise_grad(k):
            quantise(grad_q[:, k, :], grad_s[:, k, :], grad_grouped[k], E5M2)

        def turn_w2(c, b):
            k, h = divmod(b, 2)
            turn(("w2", c, b), [w2_sb[c][:, 2 * h + i, 512 * k : 512 * (k + 1)] for i in range(2)])

        def copy_w2(c, b):
            k, h = divmod(b, 2)
            grouped = once(w2_grouped, (c, k), lambda: grouped_tile("w2_grouped", 2))
            copy_turned(nc.scalar.copy, ("w2", c, b), grouped, 256 * h)

        def quantise_w2(c, k):
            codes = once(w2_q, c, lambda: tile([P, 2, CHUNK], U32, "w2_q", 2))
            scales = once(w2_s, c, lambda: tile([P, 2, CHUNK], U8, "w2_s", 2))
            quantise(codes[:, k, :], scales[:, k, :], w2_grouped[c, k], E4M3)

        def turn_w1(c, b):
            turn(("w1", c, b), [w1_sb[c][:, 2 * b + i, :] for i in range(2)])

        def copy_w1(c, b):
            grouped = once(w1_grouped, (c, b // 2), lambda: grouped_tile("w1_grouped", 2))
            copy_turned(nc.scalar.copy, ("w1", c, b), grouped, 256 * (b % 2))

        def quantise_w1(c, h):
            codes = once(w1_q, c, lambda: tile([P, D], U32, "w1_q", CHUNKS))
            scales = once(w1_s, c, lambda: tile([P, D], U8, "w1_s", CHUNKS))
            columns = slice(512 * h, 512 * (h + 1))
            quantise(codes[:, columns], scales[:, columns], w1_grouped[c, h], E4M3)

        def multiply_dh(c, t):
            dh[c, t] = dh_bank()
            for k in range(2):
                nc.tensor.matmul_mx(
                    out=dh[c, t][:],
                    lhsT=grad_q[:, k, P * t : P * (t + 1)].bitcast(E5M2),
                    lhsT_scale=grad_s[:, k, P * t : P * (t + 1)],
                    rhs=w2_q[c][:, k, :].bitcast(E4M3),
                    rhs_scale=w2_s[c][:, k, :],
                    start=(k == 0),
                    stop=(k == 1),
                )

        def gate(c, t):
            h, i = divmod(t, 2)
            out = once(gated, (c, h), lambda: tile([P, 1024], F32, "gated", 2))
            columns = slice(512 * i, 512 * (i + 1))
            nc.vector.scalar_tensor_tensor(
                out=out[:, columns], in0=tanhs[c, h][:, columns], scalar=-1.0, in1=dh[c, t][:], op0=ADD, op1=MUL
            )

        def make_dz1(c, h):
            out = once(dz1, c, lambda: tile([P, TILES, CHUNK], BF16, "dz1", 2))
            nc.vector.scalar_tensor_tensor(
                out=out[:, 2 * h : 2 * h + 2, :].rearrange("p j f -> p (j f)"),
                in0=slopes[c, h][:], scalar=-0.5, in1=gated[c, h][:], op0=ADD, op1=MUL,
            )

        def group_tokens(engine_copy, grouped, tiles):
            engine_copy(
                out=grouped[:].rearrange("p (r i) j -> p r j i", i=4),
                in_=tiles[:].rearrange("p j (r i) -> p r j i", i=4),
            )

        def group_dz1(c):
            dz1_by_token[c] = grouped_tile("dz1_by_token", 1)
            group_tokens(nc.vector.tensor_copy, dz1_by_token[c], dz1[c])

        def quantise_dz1_tokens(c):
            dz1_tok_q[c] = tile([P, CHUNK], U32, "dz1_tok_q", 3)
            dz1_tok_s[c] = tile([P, CHUNK], U8, "dz1_tok_s", 3)
            quantise(dz1_tok_q[c][:], dz1_tok_s[c][:], dz1_by_token[c], E5M2)

        def turn_dz1(c, h):
            turn(("dz1", c, h), [dz1[c][:, 2 * h + i, :] for i in range(2)])

        def copy_dz1(c, h):
            grouped = once(dz1_by_hidden, c, lambda: grouped_tile("dz1_by_hidden", 1))
            copy_turned(nc.scalar.copy, ("dz1", c, h), grouped, 256 * h)

        def quantise_dz1_hidden(c):
            dz1_hid_q[c] = tile([P, TOKENS], U32, "dz1_hid_q", CHUNKS)
            dz1_hid_s[c] = tile([P, TOKENS], U8, "dz1_hid_s", CHUNKS)
            quantise(dz1_hid_q[c][:], dz1_hid_s[c][:], dz1_by_hidden[c], E5M2)

        def centre(h, t):
            out = once(centred, (h, t // 2), lambda: tile([P, 1024], F32, "gated", 2))
            features = slice(512 * h, 512 * (h + 1))
            nc.vector.scalar_tensor_tensor(
                out=out[:, 512 * (t % 2) : 512 * (t % 2 + 1)], in0=x_sb[:, t, features],
                scalar=mean_sb[:, t : t + 1], in1=scale_all[:, features], op0=SUB, op1=MUL,
            )

        def normalise(h, t):
            out = once(xn, h, lambda: tile([P, TILES, 512], BF16, "stage", 4))
            nc.vector.scalar_tensor_tensor(
                out=out[:, t, :], in0=centred[h, t // 2][:, 512 * (t % 2) : 512 * (t % 2 + 1)],
                scalar=rstd_sb[:, t : t + 1], in1=offset_all[:, 512 * h : 512 * (h + 1)], op0=MUL, op1=ADD,
            )

        def group_xn(h):
            xn_by_token[h] = grouped_tile("stage", 4)
            group_tokens(nc.scalar.copy, xn_by_token[h], xn[h])

        def quantise_xn(h):
            features = slice(512 * h, 512 * (h + 1))
            quantise(xn_q[:, features], xn_s[:, features], xn_by_token[h], E4M3)

        def multiply_dw(c, m):
            dw[c, m] = dw_bank()
            nc.tensor.matmul_mx(
                out=dw[c, m][:],
                lhsT=xn_q[:, P * m : P * (m + 1)].bitcast(E4M3),
                lhsT_scale=xn_s[:, P * m : P * (m + 1)],
                rhs=dz1_tok_q[c][:].bitcast(E5M2),
                rhs_scale=dz1_tok_s[c][:],
                start=True,
                stop=True,
            )

        def copy_dw(c, m):
            pair = m // 2
            out = once(dw_stage, (c, pair), lambda: tile([P, 2, CHUNK], F32, "stage", 4))
            nc.scalar.copy(out=out[:, m % 2, :], in_=dw[c, m][:])
            if m % 2 == 1:
                nc.sync.dma_start(
                    out=out1_hbm[:, 2 * pair : 2 * pair + 2, c * CHUNK : (c + 1) * CHUNK], in_=out[:]
                )

        def multiply_dxn(t, h, first, last):
            group = 2 * t + h
            out = once(dxn, (t, h), lambda: turn_bank() if 3 <= group < 6 else dh_bank())
            for c in range(first, last):
                nc.tensor.matmul_mx(
                    out=out[:],
                    lhsT=dz1_hid_q[c][:, P * t : P * (t + 1)].bitcast(E5M2),
                    lhsT_scale=dz1_hid_s[c][:, P * t : P * (t + 1)],
                    rhs=w1_q[c][:, 512 * h : 512 * (h + 1)].bitcast(E4M3),
                    rhs_scale=w1_s[c][:, 512 * h : 512 * (h + 1)],
                    start=(c == 0),
                    stop=(c == CHUNKS - 1),
                )

        def scale_dxn(t, h):
            out = once(dx_scaled, t, lambda: tile([P, D], F32, "tanhs", 4))
            sums = once(dx_sums, t, lambda: tile([P, 8], F32, "dx_sums", 4))
            features = slice(512 * h, 512 * (h + 1))
            nc.vector.scalar_tensor_tensor(
                out=out[:, features], in0=dxn[t, h][:], scalar=1.0, in1=scale_all[:, features], op0=MUL, op1=MUL,
                accum_out=sums[:, h : h + 1],
            )

        def dot_dxn(t):
            products = tile([P, D], F32, "squares", 2)
            nc.vector.scalar_tensor_tensor(
                out=products[:], in0=x_sb[:, t, :], scalar=mean_sb[:, t : t + 1], in1=dx_scaled[t][:],
                op0=SUB, op1=MUL, accum_out=dx_sums[t][:, 2:3],
            )

        def coefficients(t):
            sums = dx_sums[t]
            token = slice(t, t + 1)
            second_half, slope_x, row_mean, offset_x = (sums[:, i : i + 1] for i in (3, 4, 6, 5))
            identity_of = ACT.Identity
            nc.scalar.activation(out=second_half, in_=sums[:, 1:2], func=identity_of, scale=rstd_over_d[:, token])
            nc.scalar.activation(out=slope_x, in_=sums[:, 2:3], func=identity_of, scale=rstd_cubed_over_d[:, token])
            nc.scalar.activation(
                out=row_mean, in_=sums[:, 0:1], func=identity_of, scale=rstd_over_d[:, token], bias=second_half
            )
            nc.scalar.activation(out=offset_x, in_=slope_x, func=identity_of, scale=neg_mean[:, token], bias=row_mean)

        def affine_x(t, lo, hi):
            out = once(dx_affine, t, lambda: tile([P, D], F32, "gelus", 2))
            nc.scalar.activation(
                out=out[:, lo:hi], in_=x_sb[:, t, lo:hi], func=ACT.Identity,
                scale=dx_sums[t][:, 4:5], bias=dx_sums[t][:, 5:6],
            )

        def finish_dx(t, lo, hi):
            out = once(dx_out, t, lambda: tile([P, D], F32, "slopes", 4))
            nc.vector.scalar_tensor_tensor(
                out=out[:, lo:hi], in0=dx_scaled[t][:, lo:hi], scalar=rstd_sb[:, t : t + 1],
                in1=dx_affine[t][:, lo:hi], op0=MUL, op1=SUB,
            )
            nc.sync.dma_start(out=out0_hbm[:, t, lo:hi], in_=out[:, lo:hi])

        w1_blocks = [(c, b) for c in range(CHUNKS) for b in range(4)]
        dw_blocks = [(c, m) for c in range(CHUNKS) for m in range(8)]
        queues = {
            turn_w1: w1_blocks,
            copy_w1: w1_blocks,
            quantise_w1: [(c, h) for c in range(CHUNKS) for h in range(2)],
            multiply_dw: dw_blocks,
            copy_dw: dw_blocks,
            group_xn: [(0,), (1,)],
        }

        def xn_work(piece, *args):
            piece(*args)

        queues[xn_work] = []
        for h in range(2):
            for piece, t in (
                (centre, 0), (centre, 1), (normalise, 0), (centre, 2), (normalise, 1), (centre, 3), (normalise, 2),
                (normalise, 3),
            ):
                queues[xn_work].append((piece, h, t))
            queues[xn_work].append((quantise_xn, h))
        share = {
            turn_w1: W1_BLOCKS,
            copy_w1: W1_BLOCKS,
            quantise_w1: W1_QUANTISED,
            multiply_dw: OUT1_BLOCKS,
            copy_dw: OUT1_BLOCKS,
            xn_work: XN_ITEMS,
            group_xn: XN_GROUPED,
        }
        begun = {}

        def run_next(work):
            i = begun.get(work, 0)
            begun[work] = i + 1
            work(*queues[work][i])

        def take(c, work, slot):
            if slot < share[work][c]:
                run_next(work)

        def at(work, c, *args):
            if 0 <= c < CHUNKS:
                work(c, *args)

        load_z1(0, 0)
        grad_sb = tile([P, TILES, D], BF16, "w2_sb", 2)
        for i in range(2):
            nc.sync.dma_start(out=grad_sb[:, 2 * i : 2 * i + 2, :], in_=grad_hbm[:, 2 * i : 2 * i + 2, :])
        load_z1(0, 1)
        load_w2(0)
        nc.vector.memset(table_load[:], 0.0)
        nc.scalar.activation(out=table_load[:], in_=table_load[:], func=ACT.Gelu_apprx_tanh)
        make_identity(nc, identity[:])
        nc.sync.dma_start(out=mean_sb[:], in_=mean_hbm)
        nc.sync.dma_start(out=rstd_sb[:], in_=rstd_hbm)
        nc.gpsimd.tensor_scalar(out=neg_mean[:], in0=mean_sb[:], scalar1=-1.0, scalar2=0.0, op0=MUL, op1=ADD)
        nc.gpsimd.tensor_scalar(out=rstd_over_d[:], in0=rstd_sb[:], scalar1=1.0 / D, scalar2=0.0, op0=MUL, op1=ADD)
        nc.gpsimd.tensor_tensor(out=rstd_squared[:], in0=rstd_sb[:], in1=rstd_sb[:], op=MUL)
        nc.gpsimd.tensor_tensor(out=rstd_cubed_over_d[:], in0=rstd_squared[:], in1=rstd_over_d[:], op=MUL)
        load_z1(1, 0)
        load_z1(1, 1)
        load_w2(1)
        load_w1(0)
        nc.sync.dma_start(out=x_sb[:], in_=x_hbm)
        nc.sync.dma_start(out=scale_all[:], in_=ln_scale.partition_broadcast(P))
        nc.sync.dma_start(out=offset_all[:], in_=ln_offset.partition_broadcast(P))
        load_w1(1)
        square(0, 0)
        gelu(0, 0)
        turn_grad(0, 0)
        cubic(0, 0)
        turn_grad(1, 0)
        copy_grad(0, 0, nc.scalar.copy)
        turn_grad(1, 1)
        slope(0, 0)
        turn_grad(0, 1)
        copy_grad(1, 1, nc.scalar.copy)
        copy_grad(1, 0, nc.vector.tensor_copy)
        gelu(0, 1)
        copy_grad(0, 1, nc.vector.tensor_copy)
        turn_w2(0, 2)
        quantise_grad(1)
        square(0, 1)
        turn_w2(0, 0)
        quantise_grad(0)
        turn_w2(0, 3)
        copy_w2(0, 2)
        slope(0, 1)
        copy_w2(0, 0)
        turn_w2(0, 1)
        copy_w2(0, 3)
        cubic(0, 1)
        copy_w2(0, 1)
        square(1, 0)
        quantise_w2(0, 0)
        quantise_w2(0, 1)
        multiply_dh(0, 2)
        tanh(0, 1)
        multiply_dh(0, 3)
        square(1, 1)
        turn_w2(1, 2)
        tanh(0, 0)
        gelu(1, 0)

        for c in range(CHUNKS):
            for i in (0, 1):
                at(load_z1, c + 2, i)
            at(load_w2, c + 2)
            at(load_w1, c + 2)
            at(cubic, c + 1, 0)
            at(multiply_dh, c, 1)
            at(turn_w2, c + 1, 3)
            for i in (2, 3):
                at(gate, c, i)
            at(cubic, c + 1, 1)
            at(gelu, c + 1, 1)
            at(turn_dz1, c - 1, 0)
            at(copy_w2, c + 1, 2)
            at(make_dz1, c, 1)
            at(copy_w2, c + 1, 3)
            for slot in (6, 4):
                take(c, multiply_dw, slot)
            for slot in (4, 2):
                take(c, turn_w1, slot)
            for i in (1, 0):
                at(turn_w2, c + 1, i)
            at(multiply_dh, c, 0)
            take(c, copy_dw, 1)
            at(copy_dz1, c - 1, 0)
            take(c, copy_w1, 2)
            take(c, group_xn, 1)
            take(c, quantise_w1, 3)
            at(group_dz1, c - 1)
            take(c, copy_w1, 4)
            at(slope, c + 1, 0)
            for i in (1, 0):
                at(copy_w2, c + 1, i)
            at(slope, c + 1, 1)
            at(quantise_w2, c + 1, 1)
            for slot in (4, 2):
                take(c, xn_work, slot)
            take(c, multiply_dw, 0)
            take(c, turn_w1, 5)
            take(c, multiply_dw, 9)
            for slot in (1, 0):
                take(c, turn_w1, slot)
            take(c, copy_dw, 0)
            at(tanh, c + 1, 1)
            take(c, copy_w1, 3)
            take(c, quantise_w1, 0)
            for slot in (1, 9, 6):
                take(c, xn_work, slot)
            at(quantise_w2, c + 1, 0)
            take(c, xn_work, 5)
            for slot in (1, 7):
                take(c, multiply_dw, slot)
            take(c, turn_w1, 3)
            at(turn_dz1, c, 1)
            take(c, turn_w1, 8)
            take(c, multiply_dw, 8)
            take(c, xn_work, 7)
            at(quantise_dz1_hidden, c - 1)
            take(c, turn_w1, 7)
            take(c, copy_dw, 2)
            take(c, copy_w1, 0)
            take(c, xn_work, 3)
            take(c, multiply_dw, 5)
            take(c, xn_work, 0)
            for i in (1, 0):
                at(gate, c, i)
            at(quantise_dz1_tokens, c - 1)
            take(c, turn_w1, 6)
            for i in (2, 3):
                at(multiply_dh, c + 1, i)
            at(turn_w2, c + 2, 2)
            take(c, multiply_dw, 3)
            take(c, copy_dw, 4)
            take(c, multiply_dw, 2)
            take(c, copy_dw, 3)
            at(tanh, c + 1, 0)
            for slot in (8, 9):
                take(c, copy_dw, slot)
            take(c, copy_w1, 5)
            at(square, c + 2, 0)
            take(c, copy_w1, 6)
            take(c, quantise_w1, 2)
            at(make_dz1, c, 0)
            take(c, copy_dw, 6)
            at(square, c + 2, 1)
            at(gelu, c + 2, 0)
            take(c, copy_dw, 5)
            take(c, copy_w1, 1)
            take(c, quantise_w1, 1)
            at(copy_dz1, c, 1)
            take(c, copy_dw, 7)
            take(c, group_xn, 0)
            take(c, copy_w1, 7)
            take(c, xn_work, 8)
            take(c, copy_w1, 8)

        multiply_dxn(1, 0, 0, CHUNKS - 1)
        for slot in range(2):
            run_next(multiply_dw)
        multiply_dxn(1, 1, 0, CHUNKS - 1)
        run_next(copy_dw)
        run_next(quantise_w1)
        run_next(copy_dw)
        group_dz1(5)
        run_next(multiply_dw)
        turn_dz1(5, 0)
        run_next(copy_dw)
        run_next(multiply_dw)
        copy_dz1(5, 0)
        run_next(multiply_dw)
        multiply_dxn(0, 0, 0, CHUNKS - 1)
        run_next(copy_dw)
        quantise_dz1_hidden(5)
        run_next(copy_dw)
        quantise_dz1_tokens(5)
        for slot in range(2):
            run_next(multiply_dw)
        run_next(copy_dw)
        multiply_dxn(1, 0, CHUNKS - 1, CHUNKS)
        multiply_dxn(0, 0, CHUNKS - 1, CHUNKS)
        scale_dxn(1, 0)
        run_next(copy_dw)
        multiply_dxn(1, 1, CHUNKS - 1, CHUNKS)
        run_next(multiply_dw)
        scale_dxn(1, 1)
        run_next(multiply_dw)
        run_next(copy_dw)
        multiply_dxn(3, 1, 0, CHUNKS - 1)
        run_next(copy_dw)
        dot_dxn(1)
        run_next(multiply_dw)
        scale_dxn(0, 0)
        run_next(multiply_dw)
        run_next(copy_dw)
        multiply_dxn(3, 1, CHUNKS - 1, CHUNKS)
        multiply_dxn(3, 0, 0, CHUNKS - 1)
        scale_dxn(3, 1)
        run_next(copy_dw)
        coefficients(1)
        multiply_dxn(3, 0, CHUNKS - 1, CHUNKS)
        affine_x(1, 0, D)
        run_next(multiply_dw)
        scale_dxn(3, 0)
        run_next(multiply_dw)
        multiply_dxn(0, 1, 0, CHUNKS - 1)
        run_next(copy_dw)
        dot_dxn(3)
        run_next(copy_dw)
        multiply_dxn(0, 1, CHUNKS - 1, CHUNKS)
        coefficients(3)
        finish_dx(1, 0, D)
        for slot in range(2):
            run_next(multiply_dw)
        run_next(copy_dw)
        multiply_dxn(2, 0, 0, CHUNKS - 1)
        affine_x(3, 0, D)
        scale_dxn(0, 1)
        run_next(copy_dw)
        dot_dxn(0)
        multiply_dxn(2, 0, CHUNKS - 1, CHUNKS)
        for slot in range(2):
            run_next(multiply_dw)
        run_next(copy_dw)
        multiply_dxn(2, 1, 0, CHUNKS - 1)
        scale_dxn(2, 0)
        coefficients(0)
        finish_dx(3, 0, D)
        run_next(copy_dw)
        multiply_dxn(2, 1, CHUNKS - 1, CHUNKS)
        affine_x(0, 0, D)
        run_next(multiply_dw)
        scale_dxn(2, 1)
        run_next(multiply_dw)
        dot_dxn(2)
        for slot in range(2):
            run_next(copy_dw)
        coefficients(2)
        finish_dx(0, 0, D)
        affine_x(2, 0, 512)
        affine_x(2, 512, D)
        finish_dx(2, 0, 512)
        finish_dx(2, 512, D)
